import numpy as np
import ml_dtypes


def mxq(x, axis, fmt="e4m3"):
    dtype, down = {"e4m3": (ml_dtypes.float8_e4m3fn, 7), "e5m2": (ml_dtypes.float8_e5m2, 14)}[fmt]
    v = np.moveaxis(np.asarray(x, np.float32).astype(ml_dtypes.bfloat16).astype(np.float64), axis, -1)
    blocks = v.reshape(v.shape[:-1] + (-1, 32))
    amax = np.abs(blocks).max(-1, keepdims=True)
    byte = np.maximum(np.where(amax > 0, np.frexp(amax)[1] - 1 + 127, 0) - down, 1)
    scale = np.exp2(byte - 127.0)
    codes = (blocks / scale).astype(np.float32).astype(dtype).astype(np.float64)
    return np.moveaxis((codes * scale).reshape(v.shape), -1, axis)


BF16 = ml_dtypes.bfloat16


def bf(x):
    return np.asarray(x, np.float32).astype(BF16)


def f64(x):
    return np.asarray(x).astype(np.float64)


N, M, D, R = 2048, 2048, 512, 4


def softplus(x):
    return np.logaddexp(x, 0.0)


def setup_inputs():
    basis = np.random.standard_normal((R, D)) / np.sqrt(D)
    X = 0.5 * np.random.standard_normal((N, R)) @ basis + 0.5 * np.random.standard_normal((N, D)) / np.sqrt(D)
    X2 = 0.5 * np.random.standard_normal((M, R)) @ basis + 0.5 * np.random.standard_normal((M, D)) / np.sqrt(D)
    raw1 = np.log(np.expm1(1.0))
    return {"X": bf(X), "X2": bf(X2),
            "lengthscale": bf(raw1 + 0.3 * np.random.standard_normal((1, D))),
            "variance": bf(1.5 + 0.3 * np.random.standard_normal(1))}


def reference(X, X2, lengthscale, variance):
    l = softplus(f64(lengthscale))
    v = softplus(f64(variance))
    Xl = f64(X) / l
    X2l = f64(X2) / l
    xn = np.sum(Xl * Xl, axis=1)
    yn = np.sum(X2l * X2l, axis=1)
    cross = mxq(Xl, 1, "e4m3") @ mxq(X2l, 1, "e4m3").T
    d2 = np.maximum(xn[:, None] + yn[None, :] - 2.0 * cross, 0.0)
    return v[0] * np.exp(-0.5 * d2)

@@ -1,0 +1,191 @@
+from contextlib import ExitStack
+
+import concourse.mybir as mybir
+from concourse.masks import make_identity
+
+F32 = mybir.dt.float32
+BF16 = mybir.dt.bfloat16
+U32 = mybir.dt.uint32
+U8 = mybir.dt.uint8
+FP8X4 = mybir.dt.float8_e4m3fn_x4
+ALU = mybir.AluOpType
+ACT = mybir.ActivationFunctionType
+
+P = 128
+ROWS = 2048
+D = 512
+TILES = ROWS // P
+GROUPS = TILES // 2
+GCOLS = 2 * P
+FLOPS = 2 * ROWS * ROWS * D
+
+
+def tile_rbf_kernel(tc, X, X2, lengthscale, variance, out):
+    nc = tc.nc
+    with ExitStack() as ctx:
+        const = ctx.enter_context(tc.tile_pool(name="const", bufs=1))
+        stage = ctx.enter_context(tc.tile_pool(name="stage", bufs=3))
+        work = ctx.enter_context(tc.tile_pool(name="work", bufs=4))
+        ps_tr = ctx.enter_context(tc.psum_pool(name="ps_tr", bufs=3))
+        ps_c = ctx.enter_context(tc.psum_pool(name="ps_c", bufs=4))
+        ps_n = ctx.enter_context(tc.psum_pool(name="ps_n", bufs=1))
+
+        lraw = const.tile([P, 4], BF16)
+        vraw = const.tile([P, 1], BF16)
+        nc.sync.dma_start(
+            out=lraw[:].rearrange("q (u e) -> q u e", e=2),
+            in_=lengthscale.rearrange("o (u q e) -> (o q) u e", u=2, e=2),
+        )
+        nc.sync.dma_start(out=vraw[:], in_=variance.partition_broadcast(P))
+        x2_raw = const.tile([P, TILES, D], BF16)
+        x_raw = const.tile([P, TILES, D], BF16)
+        x2_v = X2.rearrange("(c p) f -> p c f", p=P)
+        x_v = X.rearrange("(p t) f -> p t f", t=TILES)
+        out_v = out.rearrange("(p t) j -> p t j", t=TILES)
+        for raw, view, lo in (
+            (x2_raw, x2_v, 0), (x_raw, x_v, 0), (x2_raw, x2_v, 4), (x2_raw, x2_v, 8),
+            (x2_raw, x2_v, 12), (x_raw, x_v, 4), (x_raw, x_v, 8), (x_raw, x_v, 12),
+        ):
+            nc.sync.dma_start(out=raw[:, lo:lo + 4, :], in_=view[:, lo:lo + 4, :])
+
+        ident = const.tile([P, P], F32)
+        make_identity(nc, ident[:])
+
+        x5 = const.tile([P, 5], F32)
+        nc.vector.tensor_copy(out=x5[:, 0:4], in_=lraw[:])
+        nc.vector.tensor_copy(out=x5[:, 4:5], in_=vraw[:])
+        ax = const.tile([P, 5], F32)
+        nc.scalar.activation(out=ax[:], in_=x5[:], func=ACT.Abs)
+        ex = const.tile([P, 5], F32)
+        nc.scalar.activation(out=ex[:], in_=ax[:], func=ACT.Exp, scale=-1.0)
+        lp = const.tile([P, 5], F32)
+        nc.scalar.activation(out=lp[:], in_=ex[:], func=ACT.Ln, bias=1.0)
+        sp = const.tile([P, 5], F32)
+        nc.vector.scalar_tensor_tensor(out=sp[:], in0=x5[:], scalar=0.0, in1=lp[:], op0=ALU.max, op1=ALU.add)
+        rl4 = const.tile([P, 4], F32)
+        nc.vector.reciprocal(out=rl4[:], in_=sp[:, 0:4])
+        wneg = const.tile([P, 4], F32)
+        nc.vector.scalar_tensor_tensor(out=wneg[:], in0=rl4[:], scalar=-0.5, in1=rl4[:], op0=ALU.mult, op1=ALU.mult)
+        lnv = const.tile([P, 1], F32)
+        nc.scalar.activation(out=lnv[:], in_=sp[:, 4:5], func=ACT.Ln)
+        rl_b = rl4[:].rearrange("q (u e) -> q u e", e=2).unsqueeze(1).to_broadcast([P, GCOLS, 2, 2])
+
+        codes = {}
+        scls = {}
+        for name in ("x", "y"):
+            codes[name] = const.tile([P, ROWS], U32, name="codes_" + name, align_bytes=64)
+            scls[name] = const.tile([P, ROWS], U8, name="scls_" + name, align_bytes=64)
+        raws = {"x": x_raw, "y": x2_raw}
+        nrm = ps_n.tile([P, 2 * TILES], F32)
+        nbase = {"y": 0, "x": TILES}
+        half = const.tile([P, 2 * TILES], F32)
+        bcol = const.tile([P, ROWS], F32)
+        grps = {}
+
+        def prep(name, g):
+            words = raws[name][:].bitcast(F32)
+            tr = ps_tr.tile([P, 2 * GCOLS], F32, tag="tr")
+            for a in range(2):
+                for u in range(2):
+                    nc.tensor.transpose(
+                        out=tr[:, u * GCOLS + a * P:u * GCOLS + (a + 1) * P],
+                        in_=words[:, 2 * g + a, u * P:(u + 1) * P],
+                        identity=ident[:],
+                    )
+            trb = tr[:].bitcast(BF16)
+            grp = stage.tile([P, 4 * GCOLS], BF16, tag="grp", align_bytes=64)
+            nc.vector.tensor_tensor(
+                out=grp[:].rearrange("q (r u e) -> q r u e", u=2, e=2),
+                in0=trb.rearrange("q (u r e) -> q r u e", u=2, e=2),
+                in1=rl_b,
+                op=ALU.mult,
+            )
+            grps[(name, g)] = grp
+            sq = stage.tile([P, 4, GCOLS], F32, tag="sq")
+            nc.scalar.activation(
+                out=sq[:].rearrange("q (u e) r -> q u e r", e=2),
+                in_=trb.rearrange("q (u r e) -> q u e r", u=2, e=2),
+                func=ACT.Square,
+            )
+            for a in range(2):
+                col = nbase[name] + 2 * g + a
+                for ue in range(4):
+                    nc.tensor.matmul(
+                        out=nrm[:, col:col + 1],
+                        lhsT=sq[:, ue, a * P:(a + 1) * P],
+                        rhs=wneg[:, ue:ue + 1],
+                        start=(ue == 0),
+                        stop=(ue == 3),
+                    )
+
+        def quant(name, g):
+            cols = slice(g * GCOLS, (g + 1) * GCOLS)
+            nc.vector.quantize_mx(
+                out=codes[name][:, cols].bitcast(FP8X4),
+                scales=scls[name][:, cols],
+                in_=grps[(name, g)][:],
+            )
+
+        def spread(k):
+            nc.vector.tensor_copy(out=half[:, 4 * k:4 * k + 4], in_=nrm[:, 4 * k:4 * k + 4])
+            trb = ps_tr.tile([P, 2 * GCOLS], F32, tag="tr")
+            for cl in range(4):
+                nc.tensor.transpose(
+                    out=trb[:, cl * P:(cl + 1) * P],
+                    in_=half[:, 4 * k + cl:4 * k + cl + 1].to_broadcast([P, P]),
+                    identity=ident[:],
+                )
+            nc.scalar.copy(out=bcol[:, k * 512:(k + 1) * 512], in_=trb[:])
+
+        def xnorm(g):
+            lo = TILES + 2 * g
+            nc.vector.tensor_copy(out=half[:, lo:lo + 2], in_=nrm[:, lo:lo + 2])
+
+        def main(t):
+            for h in range(2):
+                arg = work.tile([P, 1024], F32, tag="arg")
+                for kk in range(2):
+                    k = 2 * h + kk
+                    acc = ps_c.tile([P, 512], F32, tag="acc")
+                    nc.tensor.matmul_mx(
+                        out=acc[:],
+                        lhsT=codes["x"][:, t * P:(t + 1) * P].bitcast(FP8X4),
+                        lhsT_scale=scls["x"][:, t * P:(t + 1) * P],
+                        rhs=codes["y"][:, k * 512:(k + 1) * 512].bitcast(FP8X4),
+                        rhs_scale=scls["y"][:, k * 512:(k + 1) * 512],
+                        start=True,
+                        stop=True,
+                    )
+                    nc.vector.scalar_tensor_tensor(
+                        out=arg[:, kk * 512:(kk + 1) * 512],
+                        in0=acc[:],
+                        scalar=half[:, TILES + t:TILES + t + 1],
+                        in1=bcol[:, k * 512:(k + 1) * 512],
+                        op0=ALU.add,
+                        op1=ALU.add,
+                    )
+                nc.gpsimd.tensor_scalar(
+                    out=arg[:], in0=arg[:], scalar1=0.0, scalar2=-3.0e38, op0=ALU.min, op1=ALU.max
+                )
+                res = work.tile([P, 1024], F32, tag="res")
+                nc.scalar.activation(out=res[:], in_=arg[:], func=ACT.Exp, bias=lnv[:, 0:1])
+                nc.sync.dma_start(out=out_v[:, t, h * 1024:(h + 1) * 1024], in_=res[:])
+
+        for g in range(GROUPS):
+            prep("y", g)
+            if g >= 1:
+                quant("y", g - 1)
+            if g % 2 == 1:
+                spread(g // 2)
+        prep("x", 0)
+        quant("y", GROUPS - 1)
+        xnorm(0)
+        quant("x", 0)
+        for g in range(GROUPS):
+            if g + 1 < GROUPS:
+                prep("x", g + 1)
+            main(2 * g)
+            if g + 1 < GROUPS:
+                xnorm(g + 1)
+                quant("x", g + 1)
+            main(2 * g + 1)

@@ -15,20 +15,23 @@ P = 128
 ROWS = 2048
 D = 512
 TILES = ROWS // P
-GROUPS = TILES // 2
 GCOLS = 2 * P
+CH = 512
+NCH = ROWS // CH
 FLOPS = 2 * ROWS * ROWS * D
 
 
 def tile_rbf_kernel(tc, X, X2, lengthscale, variance, out):
     nc = tc.nc
     with ExitStack() as ctx:
+        ctx.enter_context(tc.manual_schedule())
         const = ctx.enter_context(tc.tile_pool(name="const", bufs=1))
         stage = ctx.enter_context(tc.tile_pool(name="stage", bufs=3))
-        work = ctx.enter_context(tc.tile_pool(name="work", bufs=4))
-        ps_tr = ctx.enter_context(tc.psum_pool(name="ps_tr", bufs=3))
-        ps_c = ctx.enter_context(tc.psum_pool(name="ps_c", bufs=4))
-        ps_n = ctx.enter_context(tc.psum_pool(name="ps_n", bufs=1))
+        wpool = ctx.enter_context(tc.tile_pool(name="wpool", bufs=8))
+        rpool = ctx.enter_context(tc.tile_pool(name="rpool", bufs=3))
+        ps_acc = ctx.enter_context(tc.psum_pool(name="ps_acc", bufs=4))
+        ps_wt = ctx.enter_context(tc.psum_pool(name="ps_wt", bufs=3))
+        ps_tr = ctx.enter_context(tc.psum_pool(name="ps_tr", bufs=1))
 
         lraw = const.tile([P, 4], BF16)
         vraw = const.tile([P, 1], BF16)
@@ -43,13 +46,191 @@ def tile_rbf_kernel(tc, X, X2, lengthscale, variance, out):
         x_v = X.rearrange("(p t) f -> p t f", t=TILES)
         out_v = out.rearrange("(p t) j -> p t j", t=TILES)
         for raw, view, lo in (
-            (x2_raw, x2_v, 0), (x_raw, x_v, 0), (x2_raw, x2_v, 4), (x2_raw, x2_v, 8),
+            (x_raw, x_v, 0), (x2_raw, x2_v, 0), (x2_raw, x2_v, 4), (x2_raw, x2_v, 8),
             (x2_raw, x2_v, 12), (x_raw, x_v, 4), (x_raw, x_v, 8), (x_raw, x_v, 12),
         ):
             nc.sync.dma_start(out=raw[:, lo:lo + 4, :], in_=view[:, lo:lo + 4, :])
+        raws = {"x": x_raw, "y": x2_raw}
 
         ident = const.tile([P, P], F32)
         make_identity(nc, ident[:])
+
+        codes = {}
+        scls = {}
+        for name in ("x", "y"):
+            codes[name] = const.tile([P, ROWS], U32, name="codes_" + name, align_bytes=64)
+            scls[name] = const.tile([P, ROWS], U8, name="scls_" + name, align_bytes=64)
+        nsum = const.tile([P, 2 * TILES], F32)
+        ncol = {"y": 0, "x": TILES}
+        by = const.tile([P, TILES], F32)
+        hx = const.tile([P, TILES], F32)
+        cap = const.tile([P, ROWS], F32)
+        junk = const.tile([P, D], BF16)
+        grps = {}
+        trs = {}
+        sqs = {}
+        u32s = {}
+
+        def tpose(name, g, pool, tag):
+            words = raws[name][:].bitcast(F32)
+            tr = pool.tile([P, 2 * GCOLS], F32, tag=tag, name="tr_" + name + str(g))
+            for a in range(2):
+                for u in range(2):
+                    nc.tensor.transpose(
+                        out=tr[:, u * GCOLS + a * P:u * GCOLS + (a + 1) * P],
+                        in_=words[:, 2 * g + a, u * P:(u + 1) * P],
+                        identity=ident[:],
+                    )
+            trs[(name, g)] = tr
+
+        def scale(name, g):
+            grp = stage.tile([P, 4 * GCOLS], BF16, tag="grp", name="grp_" + name + str(g), align_bytes=64)
+            nc.vector.tensor_tensor(
+                out=grp[:].rearrange("q (r u e) -> q r u e", u=2, e=2),
+                in0=trs[(name, g)][:].bitcast(BF16).rearrange("q (u r e) -> q r u e", u=2, e=2),
+                in1=rl4[:].rearrange("q (u e) -> q u e", e=2).unsqueeze(1).to_broadcast([P, GCOLS, 2, 2]),
+                op=ALU.mult,
+            )
+            grps[(name, g)] = grp
+
+        def square(name, g):
+            sq = stage.tile([P, 4, GCOLS], F32, tag="sq", name="sq_" + name + str(g))
+            nc.scalar.activation(
+                out=sq[:].rearrange("q (u e) r -> q u e r", e=2),
+                in_=trs[(name, g)][:].bitcast(BF16).rearrange("q (u r e) -> q u e r", u=2, e=2),
+                func=ACT.Square,
+            )
+            sqs[(name, g)] = sq
+
+        def matvec(name, g, nrm, col):
+            for a in range(2):
+                for ue in range(4):
+                    nc.tensor.matmul(
+                        out=nrm[:, col + a:col + a + 1],
+                        lhsT=sqs[(name, g)][:, ue, a * P:(a + 1) * P],
+                        rhs=wneg[:, ue:ue + 1],
+                        start=(ue == 0),
+                        stop=(ue == 3),
+                    )
+
+        def quant(name, g):
+            cols = slice(g * GCOLS, (g + 1) * GCOLS)
+            nc.vector.quantize_mx(
+                out=codes[name][:, cols].bitcast(FP8X4),
+                scales=scls[name][:, cols],
+                in_=grps[(name, g)][:],
+            )
+
+        def fin_psum(name, ch, nrm, col):
+            if name == "y":
+                nc.vector.tensor_scalar(
+                    out=by[:, 4 * ch:4 * ch + 4], in0=nrm[:, col:col + 4], scalar1=lnv[:, 0:1], scalar2=None, op0=ALU.add
+                )
+            else:
+                nc.vector.tensor_copy(out=hx[:, 4 * ch:4 * ch + 4], in_=nrm[:, col:col + 4])
+
+        def rows_scaled(name, g):
+            u32 = const.tile([P, 2, D], F32, name="u32_" + name + str(g))
+            nc.gpsimd.tensor_tensor(
+                out=u32[:],
+                in0=raws[name][:, 2 * g:2 * g + 2, :],
+                in1=rlb[:].unsqueeze(1).to_broadcast([P, 2, D]),
+                op=ALU.mult,
+            )
+            u32s[(name, g)] = u32
+
+        def row_norms(name, g):
+            for a in range(2):
+                col = ncol[name] + 2 * g + a
+                nc.scalar.activation(
+                    out=junk[:], in_=u32s[(name, g)][:, a, :], func=ACT.Square, accum_out=nsum[:, col:col + 1]
+                )
+
+        def fin_pool(name, ch):
+            lo = ncol[name] + 4 * ch
+            if name == "y":
+                nc.vector.tensor_scalar(
+                    out=by[:, 4 * ch:4 * ch + 4], in0=nsum[:, lo:lo + 4], scalar1=-0.5, scalar2=lnv[:, 0:1],
+                    op0=ALU.mult, op1=ALU.add,
+                )
+            else:
+                nc.vector.tensor_scalar(
+                    out=hx[:, 4 * ch:4 * ch + 4], in0=nsum[:, lo:lo + 4], scalar1=-0.5, scalar2=None, op0=ALU.mult
+                )
+
+        def spread(ch, pool, tag):
+            sp_ps = pool.tile([P, CH], F32, tag=tag, name="spread" + str(ch))
+            for tl in range(4):
+                nc.tensor.transpose(
+                    out=sp_ps[:, tl * P:(tl + 1) * P],
+                    in_=hx[:, 4 * ch + tl:4 * ch + tl + 1].to_broadcast([P, P]),
+                    identity=ident[:],
+                )
+            nc.scalar.activation(
+                out=cap[:, ch * CH:(ch + 1) * CH], in_=sp_ps[:], func=ACT.Identity, bias=lnv[:, 0:1], scale=-1.0
+            )
+
+        accs = {}
+        wts = {}
+        ws = {}
+        ress = {}
+
+        def mx(s):
+            i_ch, k_ch = divmod(s, NCH)
+            for cl in range(4):
+                c = 4 * k_ch + cl
+                acc = ps_acc.tile([P, CH], F32, tag="acc", name="acc" + str(s) + "_" + str(cl))
+                nc.tensor.matmul_mx(
+                    out=acc[:],
+                    lhsT=codes["y"][:, c * P:(c + 1) * P].bitcast(FP8X4),
+                    lhsT_scale=scls["y"][:, c * P:(c + 1) * P],
+                    rhs=codes["x"][:, i_ch * CH:(i_ch + 1) * CH].bitcast(FP8X4),
+                    rhs_scale=scls["x"][:, i_ch * CH:(i_ch + 1) * CH],
+                    start=True,
+                    stop=True,
+                )
+                accs[(s, cl)] = acc
+
+        def stt(s, cls):
+            i_ch, k_ch = divmod(s, NCH)
+            for cl in cls:
+                c = 4 * k_ch + cl
+                w = wpool.tile([P, CH], F32, tag="w", name="w" + str(s) + "_" + str(cl))
+                nc.vector.scalar_tensor_tensor(
+                    out=w[:],
+                    in0=accs[(s, cl)][:],
+                    scalar=by[:, c:c + 1],
+                    in1=cap[:, i_ch * CH:(i_ch + 1) * CH],
+                    op0=ALU.add,
+                    op1=ALU.min,
+                )
+                ws[(s, cl)] = w
+
+        def tp4(s, tl):
+            wt = ps_wt.tile([P, CH], F32, tag="wt", name="wt" + str(s) + "_" + str(tl))
+            for cl in range(4):
+                nc.tensor.transpose(
+                    out=wt[:, cl * P:(cl + 1) * P], in_=ws[(s, cl)][:, tl * P:(tl + 1) * P], identity=ident[:]
+                )
+            wts[(s, tl)] = wt
+
+        def expo(s, tl):
+            i_ch, k_ch = divmod(s, NCH)
+            t = 4 * i_ch + tl
+            if k_ch % 2 == 0:
+                ress[tl] = rpool.tile([P, 2 * CH], F32, tag="res" + str(tl), name="res" + str(s) + "_" + str(tl))
+            res = ress[tl]
+            lo = (k_ch % 2) * CH
+            nc.scalar.activation(
+                out=res[:, lo:lo + CH], in_=wts[(s, tl)][:], func=ACT.Exp, bias=hx[:, t:t + 1]
+            )
+            if k_ch % 2 == 1:
+                nc.sync.dma_start(out=out_v[:, t, (k_ch - 1) * CH:(k_ch + 1) * CH], in_=res[:])
+
+        for name, g in (("x", 0), ("x", 1), ("y", 0), ("y", 1)):
+            tpose(name, g, ps_acc, "acc")
+        tpose("y", 2, ps_tr, "tr")
+        tpose("y", 3, ps_wt, "wt")
 
         x5 = const.tile([P, 5], F32)
         nc.vector.tensor_copy(out=x5[:, 0:4], in_=lraw[:])
@@ -66,126 +247,86 @@ def tile_rbf_kernel(tc, X, X2, lengthscale, variance, out):
         nc.vector.reciprocal(out=rl4[:], in_=sp[:, 0:4])
         wneg = const.tile([P, 4], F32)
         nc.vector.scalar_tensor_tensor(out=wneg[:], in0=rl4[:], scalar=-0.5, in1=rl4[:], op0=ALU.mult, op1=ALU.mult)
+        square("x", 0)
         lnv = const.tile([P, 1], F32)
         nc.scalar.activation(out=lnv[:], in_=sp[:, 4:5], func=ACT.Ln)
-        rl_b = rl4[:].rearrange("q (u e) -> q u e", e=2).unsqueeze(1).to_broadcast([P, GCOLS, 2, 2])
 
-        codes = {}
-        scls = {}
-        for name in ("x", "y"):
-            codes[name] = const.tile([P, ROWS], U32, name="codes_" + name, align_bytes=64)
-            scls[name] = const.tile([P, ROWS], U8, name="scls_" + name, align_bytes=64)
-        raws = {"x": x_raw, "y": x2_raw}
-        nrm = ps_n.tile([P, 2 * TILES], F32)
-        nbase = {"y": 0, "x": TILES}
-        half = const.tile([P, 2 * TILES], F32)
-        bcol = const.tile([P, ROWS], F32)
-        grps = {}
-
-        def prep(name, g):
-            words = raws[name][:].bitcast(F32)
-            tr = ps_tr.tile([P, 2 * GCOLS], F32, tag="tr")
-            for a in range(2):
-                for u in range(2):
-                    nc.tensor.transpose(
-                        out=tr[:, u * GCOLS + a * P:u * GCOLS + (a + 1) * P],
-                        in_=words[:, 2 * g + a, u * P:(u + 1) * P],
-                        identity=ident[:],
-                    )
-            trb = tr[:].bitcast(BF16)
-            grp = stage.tile([P, 4 * GCOLS], BF16, tag="grp", align_bytes=64)
-            nc.vector.tensor_tensor(
-                out=grp[:].rearrange("q (r u e) -> q r u e", u=2, e=2),
-                in0=trb.rearrange("q (u r e) -> q r u e", u=2, e=2),
-                in1=rl_b,
-                op=ALU.mult,
+        rlt = ps_wt.tile([P, CH], F32, tag="wt")
+        for ue in range(4):
+            nc.tensor.transpose(
+                out=rlt[:, ue * P:(ue + 1) * P], in_=rl4[:, ue:ue + 1].to_broadcast([P, P]), identity=ident[:]
             )
-            grps[(name, g)] = grp
-            sq = stage.tile([P, 4, GCOLS], F32, tag="sq")
-            nc.scalar.activation(
-                out=sq[:].rearrange("q (u e) r -> q u e r", e=2),
-                in_=trb.rearrange("q (u r e) -> q u e r", u=2, e=2),
-                func=ACT.Square,
-            )
-            for a in range(2):
-                col = nbase[name] + 2 * g + a
-                for ue in range(4):
-                    nc.tensor.matmul(
-                        out=nrm[:, col:col + 1],
-                        lhsT=sq[:, ue, a * P:(a + 1) * P],
-                        rhs=wneg[:, ue:ue + 1],
-                        start=(ue == 0),
-                        stop=(ue == 3),
-                    )
+        rlb = const.tile([P, D], F32)
+        nc.scalar.copy(
+            out=rlb[:].rearrange("m (u q e) -> m u q e", u=2, e=2),
+            in_=rlt[:].rearrange("m (u e q) -> m u q e", u=2, e=2),
+        )
+        for name, g in (("y", 4), ("y", 5), ("y", 6), ("y", 7), ("x", 2), ("x", 3), ("x", 4), ("x", 5), ("x", 6), ("x", 7)):
+            rows_scaled(name, g)
 
-        def quant(name, g):
-            cols = slice(g * GCOLS, (g + 1) * GCOLS)
-            nc.vector.quantize_mx(
-                out=codes[name][:, cols].bitcast(FP8X4),
-                scales=scls[name][:, cols],
-                in_=grps[(name, g)][:],
-            )
-
-        def spread(k):
-            nc.vector.tensor_copy(out=half[:, 4 * k:4 * k + 4], in_=nrm[:, 4 * k:4 * k + 4])
-            trb = ps_tr.tile([P, 2 * GCOLS], F32, tag="tr")
-            for cl in range(4):
-                nc.tensor.transpose(
-                    out=trb[:, cl * P:(cl + 1) * P],
-                    in_=half[:, 4 * k + cl:4 * k + cl + 1].to_broadcast([P, P]),
-                    identity=ident[:],
-                )
-            nc.scalar.copy(out=bcol[:, k * 512:(k + 1) * 512], in_=trb[:])
-
-        def xnorm(g):
-            lo = TILES + 2 * g
-            nc.vector.tensor_copy(out=half[:, lo:lo + 2], in_=nrm[:, lo:lo + 2])
-
-        def main(t):
-            for h in range(2):
-                arg = work.tile([P, 1024], F32, tag="arg")
-                for kk in range(2):
-                    k = 2 * h + kk
-                    acc = ps_c.tile([P, 512], F32, tag="acc")
-                    nc.tensor.matmul_mx(
-                        out=acc[:],
-                        lhsT=codes["x"][:, t * P:(t + 1) * P].bitcast(FP8X4),
-                        lhsT_scale=scls["x"][:, t * P:(t + 1) * P],
-                        rhs=codes["y"][:, k * 512:(k + 1) * 512].bitcast(FP8X4),
-                        rhs_scale=scls["y"][:, k * 512:(k + 1) * 512],
-                        start=True,
-                        stop=True,
-                    )
-                    nc.vector.scalar_tensor_tensor(
-                        out=arg[:, kk * 512:(kk + 1) * 512],
-                        in0=acc[:],
-                        scalar=half[:, TILES + t:TILES + t + 1],
-                        in1=bcol[:, k * 512:(k + 1) * 512],
-                        op0=ALU.add,
-                        op1=ALU.add,
-                    )
-                nc.gpsimd.tensor_scalar(
-                    out=arg[:], in0=arg[:], scalar1=0.0, scalar2=-3.0e38, op0=ALU.min, op1=ALU.max
-                )
-                res = work.tile([P, 1024], F32, tag="res")
-                nc.scalar.activation(out=res[:], in_=arg[:], func=ACT.Exp, bias=lnv[:, 0:1])
-                nc.sync.dma_start(out=out_v[:, t, h * 1024:(h + 1) * 1024], in_=res[:])
-
-        for g in range(GROUPS):
-            prep("y", g)
-            if g >= 1:
-                quant("y", g - 1)
-            if g % 2 == 1:
-                spread(g // 2)
-        prep("x", 0)
-        quant("y", GROUPS - 1)
-        xnorm(0)
+        nrm0 = ps_wt.tile([P, CH], F32, tag="wt")
+        scale("x", 0)
+        square("x", 1)
+        scale("x", 1)
+        matvec("x", 0, nrm0, 0)
         quant("x", 0)
-        for g in range(GROUPS):
-            if g + 1 < GROUPS:
-                prep("x", g + 1)
-            main(2 * g)
-            if g + 1 < GROUPS:
-                xnorm(g + 1)
-                quant("x", g + 1)
-            main(2 * g + 1)
+        square("y", 0)
+        scale("y", 0)
+        matvec("x", 1, nrm0, 2)
+        quant("x", 1)
+        fin_psum("x", 0, nrm0, 0)
+        spread(0, ps_acc, "acc")
+        square("y", 1)
+        scale("y", 1)
+        matvec("y", 0, nrm0, 4)
+        quant("y", 0)
+        matvec("y", 1, nrm0, 6)
+        quant("y", 1)
+        fin_psum("y", 0, nrm0, 4)
+
+        plan = {
+            0: (("y", 2), ("y", 3)), 1: (("y", 4), ("y", 5)), 2: (("y", 6), ("y", 7)), 3: (("x", 2), ("x", 3)),
+            4: (("x", 4),), 6: (("x", 5),), 8: (("x", 6),), 10: (("x", 7),),
+        }
+        norms_at = {
+            0: (("y", 4), ("y", 5)), 1: (("y", 6), ("y", 7)), 2: (("x", 2), ("x", 3)),
+            4: (("x", 4),), 5: (("x", 5),), 8: (("x", 6),), 9: (("x", 7),),
+        }
+        steps = NCH * NCH
+        for s in range(steps + 1):
+            cur = plan.get(s, ())
+            nxt = plan.get(s + 1, ())
+            if s == 1:
+                fin_psum("y", 1, nrm0, 8)
+            if s in (2, 3):
+                fin_pool("y", s)
+            if s in (3, 7, 11):
+                fin_pool("x", (s + 1) // 4)
+                spread((s + 1) // 4, ps_wt, "wt")
+            if s < steps:
+                mx(s)
+            if s == 0:
+                square("y", 2)
+                square("y", 3)
+                matvec("y", 2, nrm0, 8)
+                matvec("y", 3, nrm0, 10)
+            if len(cur) > 0:
+                scale(cur[0][0], cur[0][1])
+            if len(cur) > 1 and s > 0:
+                tpose(cur[1][0], cur[1][1], ps_tr, "tr")
+            if s < steps:
+                stt(s, (0, 1))
+            if len(cur) > 1:
+                scale(cur[1][0], cur[1][1])
+            if s > 0:
+                for tl in range(4):
+                    tp4(s - 1, tl)
+                    expo(s - 1, tl)
+            for name, g in norms_at.get(s, ()):
+                row_norms(name, g)
+            if len(nxt) > 0:
+                tpose(nxt[0][0], nxt[0][1], ps_tr, "tr")
+            if s < steps:
+                stt(s, (2, 3))
+            for name, g in cur:
+                quant(name, g)

@@ -231,6 +231,7 @@ def tile_rbf_kernel(tc, X, X2, lengthscale, variance, out):
             tpose(name, g, ps_acc, "acc")
         tpose("y", 2, ps_tr, "tr")
         tpose("y", 3, ps_wt, "wt")
+        tpose("y", 4, ps_wt, "wt")
 
         x5 = const.tile([P, 5], F32)
         nc.vector.tensor_copy(out=x5[:, 0:4], in_=lraw[:])
@@ -247,7 +248,6 @@ def tile_rbf_kernel(tc, X, X2, lengthscale, variance, out):
         nc.vector.reciprocal(out=rl4[:], in_=sp[:, 0:4])
         wneg = const.tile([P, 4], F32)
         nc.vector.scalar_tensor_tensor(out=wneg[:], in0=rl4[:], scalar=-0.5, in1=rl4[:], op0=ALU.mult, op1=ALU.mult)
-        square("x", 0)
         lnv = const.tile([P, 1], F32)
         nc.scalar.activation(out=lnv[:], in_=sp[:, 4:5], func=ACT.Ln)
 
@@ -261,58 +261,58 @@ def tile_rbf_kernel(tc, X, X2, lengthscale, variance, out):
             out=rlb[:].rearrange("m (u q e) -> m u q e", u=2, e=2),
             in_=rlt[:].rearrange("m (u e q) -> m u q e", u=2, e=2),
         )
-        for name, g in (("y", 4), ("y", 5), ("y", 6), ("y", 7), ("x", 2), ("x", 3), ("x", 4), ("x", 5), ("x", 6), ("x", 7)):
+        order = (
+            ("x", 0), ("x", 1), ("y", 0), ("y", 1), ("y", 2), ("y", 3), ("y", 4), ("y", 5),
+            ("y", 6), ("y", 7), ("x", 2), ("x", 3), ("x", 4), ("x", 5), ("x", 6), ("x", 7),
+        )
+        for name, g in order:
             rows_scaled(name, g)
 
-        nrm0 = ps_wt.tile([P, CH], F32, tag="wt")
         scale("x", 0)
-        square("x", 1)
         scale("x", 1)
-        matvec("x", 0, nrm0, 0)
         quant("x", 0)
-        square("y", 0)
         scale("y", 0)
-        matvec("x", 1, nrm0, 2)
         quant("x", 1)
-        fin_psum("x", 0, nrm0, 0)
-        spread(0, ps_acc, "acc")
-        square("y", 1)
         scale("y", 1)
-        matvec("y", 0, nrm0, 4)
         quant("y", 0)
-        matvec("y", 1, nrm0, 6)
+        scale("y", 2)
+        tpose("y", 6, ps_tr, "tr")
         quant("y", 1)
-        fin_psum("y", 0, nrm0, 4)
+        scale("y", 3)
+        tpose("y", 5, ps_wt, "wt")
+        quant("y", 2)
+        row_norms("x", 0)
+        row_norms("x", 1)
+        scale("y", 4)
+        quant("y", 3)
+        fin_pool("x", 0)
+        spread(0, ps_acc, "acc")
+        scale("y", 5)
+        quant("y", 4)
+        quant("y", 5)
+        row_norms("y", 0)
+        row_norms("y", 1)
+        fin_pool("y", 0)
 
-        plan = {
-            0: (("y", 2), ("y", 3)), 1: (("y", 4), ("y", 5)), 2: (("y", 6), ("y", 7)), 3: (("x", 2), ("x", 3)),
-            4: (("x", 4),), 6: (("x", 5),), 8: (("x", 6),), 10: (("x", 7),),
-        }
+        plan = {0: (("y", 6), ("y", 7)), 1: (("x", 2),), 2: (("x", 3),), 3: (("x", 4),), 4: (("x", 5),), 5: (("x", 6),), 6: (("x", 7),)}
         norms_at = {
-            0: (("y", 4), ("y", 5)), 1: (("y", 6), ("y", 7)), 2: (("x", 2), ("x", 3)),
-            4: (("x", 4),), 5: (("x", 5),), 8: (("x", 6),), 9: (("x", 7),),
+            0: (("y", 2), ("y", 3)), 1: (("y", 4), ("y", 5)), 2: (("y", 6), ("y", 7)), 3: (("x", 2), ("x", 3)),
+            4: (("x", 4), ("x", 5)), 5: (("x", 6),), 6: (("x", 7),),
         }
         steps = NCH * NCH
         for s in range(steps + 1):
             cur = plan.get(s, ())
             nxt = plan.get(s + 1, ())
-            if s == 1:
-                fin_psum("y", 1, nrm0, 8)
-            if s in (2, 3):
+            if s in (1, 2, 3):
                 fin_pool("y", s)
-            if s in (3, 7, 11):
+            if s in (4, 7, 11):
                 fin_pool("x", (s + 1) // 4)
                 spread((s + 1) // 4, ps_wt, "wt")
             if s < steps:
                 mx(s)
-            if s == 0:
-                square("y", 2)
-                square("y", 3)
-                matvec("y", 2, nrm0, 8)
-                matvec("y", 3, nrm0, 10)
             if len(cur) > 0:
                 scale(cur[0][0], cur[0][1])
-            if len(cur) > 1 and s > 0:
+            if len(cur) > 1:
                 tpose(cur[1][0], cur[1][1], ps_tr, "tr")
             if s < steps:
                 stt(s, (0, 1))

@@ -43,8 +43,8 @@ def tile_rbf_kernel(tc, X, X2, lengthscale, variance, out):
         x2_raw = const.tile([P, TILES, D], BF16)
         x_raw = const.tile([P, TILES, D], BF16)
         x2_v = X2.rearrange("(c p) f -> p c f", p=P)
-        x_v = X.rearrange("(p t) f -> p t f", t=TILES)
-        out_v = out.rearrange("(p t) j -> p t j", t=TILES)
+        x_v = X.rearrange("(t p) f -> p t f", p=P)
+        out_v = out.rearrange("(t p) j -> p t j", p=P)
         for raw, view, lo in (
             (x_raw, x_v, 0), (x2_raw, x2_v, 0), (x2_raw, x2_v, 4), (x2_raw, x2_v, 8),
             (x2_raw, x2_v, 12), (x_raw, x_v, 4), (x_raw, x_v, 8), (x_raw, x_v, 12),

@@ -17,8 +17,9 @@ D = 512
 TILES = ROWS // P
 GCOLS = 2 * P
 CH = 512
-NCH = ROWS // CH
+UNIT = 2 * CH
 FLOPS = 2 * ROWS * ROWS * D
+LAG = 3
 
 
 def tile_rbf_kernel(tc, X, X2, lengthscale, variance, out):
@@ -27,11 +28,10 @@ def tile_rbf_kernel(tc, X, X2, lengthscale, variance, out):
         ctx.enter_context(tc.manual_schedule())
         const = ctx.enter_context(tc.tile_pool(name="const", bufs=1))
         stage = ctx.enter_context(tc.tile_pool(name="stage", bufs=3))
-        wpool = ctx.enter_context(tc.tile_pool(name="wpool", bufs=8))
-        rpool = ctx.enter_context(tc.tile_pool(name="rpool", bufs=3))
+        apool = ctx.enter_context(tc.tile_pool(name="apool", bufs=8))
+        rpool = ctx.enter_context(tc.tile_pool(name="rpool", bufs=4))
         ps_acc = ctx.enter_context(tc.psum_pool(name="ps_acc", bufs=4))
-        ps_wt = ctx.enter_context(tc.psum_pool(name="ps_wt", bufs=3))
-        ps_tr = ctx.enter_context(tc.psum_pool(name="ps_tr", bufs=1))
+        ps_tr = ctx.enter_context(tc.psum_pool(name="ps_tr", bufs=4))
 
         lraw = const.tile([P, 4], BF16)
         vraw = const.tile([P, 1], BF16)
@@ -46,8 +46,8 @@ def tile_rbf_kernel(tc, X, X2, lengthscale, variance, out):
         x_v = X.rearrange("(t p) f -> p t f", p=P)
         out_v = out.rearrange("(t p) j -> p t j", p=P)
         for raw, view, lo in (
-            (x_raw, x_v, 0), (x2_raw, x2_v, 0), (x2_raw, x2_v, 4), (x2_raw, x2_v, 8),
-            (x2_raw, x2_v, 12), (x_raw, x_v, 4), (x_raw, x_v, 8), (x_raw, x_v, 12),
+            (x2_raw, x2_v, 0), (x2_raw, x2_v, 4), (x_raw, x_v, 0), (x_raw, x_v, 4),
+            (x_raw, x_v, 8), (x_raw, x_v, 12), (x2_raw, x2_v, 8), (x2_raw, x2_v, 12),
         ):
             nc.sync.dma_start(out=raw[:, lo:lo + 4, :], in_=view[:, lo:lo + 4, :])
         raws = {"x": x_raw, "y": x2_raw}
@@ -60,20 +60,18 @@ def tile_rbf_kernel(tc, X, X2, lengthscale, variance, out):
         for name in ("x", "y"):
             codes[name] = const.tile([P, ROWS], U32, name="codes_" + name, align_bytes=64)
             scls[name] = const.tile([P, ROWS], U8, name="scls_" + name, align_bytes=64)
-        nsum = const.tile([P, 2 * TILES], F32)
         ncol = {"y": 0, "x": TILES}
-        by = const.tile([P, TILES], F32)
-        hx = const.tile([P, TILES], F32)
-        cap = const.tile([P, ROWS], F32)
+        nsum = const.tile([P, 2 * TILES], F32)
+        half = const.tile([P, 2 * TILES], F32)
         junk = const.tile([P, D], BF16)
+        nb = const.tile([P, ROWS], F32)
         grps = {}
         trs = {}
-        sqs = {}
         u32s = {}
 
-        def tpose(name, g, pool, tag):
+        def tpose(name, g):
             words = raws[name][:].bitcast(F32)
-            tr = pool.tile([P, 2 * GCOLS], F32, tag=tag, name="tr_" + name + str(g))
+            tr = ps_tr.tile([P, 2 * GCOLS], F32, tag="tr", name="tr_" + name + str(g))
             for a in range(2):
                 for u in range(2):
                     nc.tensor.transpose(
@@ -93,26 +91,6 @@ def tile_rbf_kernel(tc, X, X2, lengthscale, variance, out):
             )
             grps[(name, g)] = grp
 
-        def square(name, g):
-            sq = stage.tile([P, 4, GCOLS], F32, tag="sq", name="sq_" + name + str(g))
-            nc.scalar.activation(
-                out=sq[:].rearrange("q (u e) r -> q u e r", e=2),
-                in_=trs[(name, g)][:].bitcast(BF16).rearrange("q (u r e) -> q u e r", u=2, e=2),
-                func=ACT.Square,
-            )
-            sqs[(name, g)] = sq
-
-        def matvec(name, g, nrm, col):
-            for a in range(2):
-                for ue in range(4):
-                    nc.tensor.matmul(
-                        out=nrm[:, col + a:col + a + 1],
-                        lhsT=sqs[(name, g)][:, ue, a * P:(a + 1) * P],
-                        rhs=wneg[:, ue:ue + 1],
-                        start=(ue == 0),
-                        stop=(ue == 3),
-                    )
-
         def quant(name, g):
             cols = slice(g * GCOLS, (g + 1) * GCOLS)
             nc.vector.quantize_mx(
@@ -120,14 +98,6 @@ def tile_rbf_kernel(tc, X, X2, lengthscale, variance, out):
                 scales=scls[name][:, cols],
                 in_=grps[(name, g)][:],
             )
-
-        def fin_psum(name, ch, nrm, col):
-            if name == "y":
-                nc.vector.tensor_scalar(
-                    out=by[:, 4 * ch:4 * ch + 4], in0=nrm[:, col:col + 4], scalar1=lnv[:, 0:1], scalar2=None, op0=ALU.add
-                )
-            else:
-                nc.vector.tensor_copy(out=hx[:, 4 * ch:4 * ch + 4], in_=nrm[:, col:col + 4])
 
         def rows_scaled(name, g):
             u32 = const.tile([P, 2, D], F32, name="u32_" + name + str(g))
@@ -146,92 +116,68 @@ def tile_rbf_kernel(tc, X, X2, lengthscale, variance, out):
                     out=junk[:], in_=u32s[(name, g)][:, a, :], func=ACT.Square, accum_out=nsum[:, col:col + 1]
                 )
 
-        def fin_pool(name, ch):
-            lo = ncol[name] + 4 * ch
-            if name == "y":
-                nc.vector.tensor_scalar(
-                    out=by[:, 4 * ch:4 * ch + 4], in0=nsum[:, lo:lo + 4], scalar1=-0.5, scalar2=lnv[:, 0:1],
-                    op0=ALU.mult, op1=ALU.add,
-                )
-            else:
-                nc.vector.tensor_scalar(
-                    out=hx[:, 4 * ch:4 * ch + 4], in0=nsum[:, lo:lo + 4], scalar1=-0.5, scalar2=None, op0=ALU.mult
-                )
+        def fetch(lo, n):
+            nc.vector.tensor_scalar(out=half[:, lo:lo + n], in0=nsum[:, lo:lo + n], scalar1=-0.5, scalar2=None, op0=ALU.mult)
 
-        def spread(ch, pool, tag):
-            sp_ps = pool.tile([P, CH], F32, tag=tag, name="spread" + str(ch))
-            for tl in range(4):
+        def spread(k, pool, tag):
+            sp_ps = pool.tile([P, CH], F32, tag=tag, name="spread" + str(k))
+            for cl in range(4):
                 nc.tensor.transpose(
-                    out=sp_ps[:, tl * P:(tl + 1) * P],
-                    in_=hx[:, 4 * ch + tl:4 * ch + tl + 1].to_broadcast([P, P]),
+                    out=sp_ps[:, cl * P:(cl + 1) * P],
+                    in_=half[:, 4 * k + cl:4 * k + cl + 1].to_broadcast([P, P]),
                     identity=ident[:],
                 )
-            nc.scalar.activation(
-                out=cap[:, ch * CH:(ch + 1) * CH], in_=sp_ps[:], func=ACT.Identity, bias=lnv[:, 0:1], scale=-1.0
-            )
+            nc.scalar.mul(out=nb[:, k * CH:(k + 1) * CH], in_=sp_ps[:], mul=-1.0)
 
         accs = {}
-        wts = {}
-        ws = {}
-        ress = {}
+        args = {}
 
-        def mx(s):
-            i_ch, k_ch = divmod(s, NCH)
-            for cl in range(4):
-                c = 4 * k_ch + cl
-                acc = ps_acc.tile([P, CH], F32, tag="acc", name="acc" + str(s) + "_" + str(cl))
+        def mxu(t, h):
+            for kk in range(2):
+                k = 2 * h + kk
+                acc = ps_acc.tile([P, CH], F32, tag="acc", name="acc" + str(t) + "_" + str(k))
                 nc.tensor.matmul_mx(
                     out=acc[:],
-                    lhsT=codes["y"][:, c * P:(c + 1) * P].bitcast(FP8X4),
-                    lhsT_scale=scls["y"][:, c * P:(c + 1) * P],
-                    rhs=codes["x"][:, i_ch * CH:(i_ch + 1) * CH].bitcast(FP8X4),
-                    rhs_scale=scls["x"][:, i_ch * CH:(i_ch + 1) * CH],
+                    lhsT=codes["x"][:, t * P:(t + 1) * P].bitcast(FP8X4),
+                    lhsT_scale=scls["x"][:, t * P:(t + 1) * P],
+                    rhs=codes["y"][:, k * CH:(k + 1) * CH].bitcast(FP8X4),
+                    rhs_scale=scls["y"][:, k * CH:(k + 1) * CH],
                     start=True,
                     stop=True,
                 )
-                accs[(s, cl)] = acc
+                accs[(t, k)] = acc
 
-        def stt(s, cls):
-            i_ch, k_ch = divmod(s, NCH)
-            for cl in cls:
-                c = 4 * k_ch + cl
-                w = wpool.tile([P, CH], F32, tag="w", name="w" + str(s) + "_" + str(cl))
+        def addu(t, h, on_pool):
+            arg = apool.tile([P, UNIT], F32, tag="arg", name="arg" + str(t) + "_" + str(h))
+            for kk in range(2):
+                k = 2 * h + kk
                 nc.vector.scalar_tensor_tensor(
-                    out=w[:],
-                    in0=accs[(s, cl)][:],
-                    scalar=by[:, c:c + 1],
-                    in1=cap[:, i_ch * CH:(i_ch + 1) * CH],
+                    out=arg[:, kk * CH:(kk + 1) * CH],
+                    in0=accs[(t, k)][:],
+                    scalar=half[:, TILES + t:TILES + t + 1],
+                    in1=nb[:, k * CH:(k + 1) * CH],
                     op0=ALU.add,
-                    op1=ALU.min,
+                    op1=(ALU.min if on_pool else ALU.subtract),
                 )
-                ws[(s, cl)] = w
+            args[(t, h)] = arg
+            if on_pool:
+                nc.gpsimd.tensor_tensor(out=arg[:], in0=arg[:], in1=nb[:, h * UNIT:(h + 1) * UNIT], op=ALU.subtract)
 
-        def tp4(s, tl):
-            wt = ps_wt.tile([P, CH], F32, tag="wt", name="wt" + str(s) + "_" + str(tl))
-            for cl in range(4):
-                nc.tensor.transpose(
-                    out=wt[:, cl * P:(cl + 1) * P], in_=ws[(s, cl)][:, tl * P:(tl + 1) * P], identity=ident[:]
-                )
-            wts[(s, tl)] = wt
+        def clamp(t, h):
+            arg = args[(t, h)]
+            nc.vector.tensor_scalar(out=arg[:], in0=arg[:], scalar1=0.0, scalar2=None, op0=ALU.min)
 
-        def expo(s, tl):
-            i_ch, k_ch = divmod(s, NCH)
-            t = 4 * i_ch + tl
-            if k_ch % 2 == 0:
-                ress[tl] = rpool.tile([P, 2 * CH], F32, tag="res" + str(tl), name="res" + str(s) + "_" + str(tl))
-            res = ress[tl]
-            lo = (k_ch % 2) * CH
-            nc.scalar.activation(
-                out=res[:, lo:lo + CH], in_=wts[(s, tl)][:], func=ACT.Exp, bias=hx[:, t:t + 1]
-            )
-            if k_ch % 2 == 1:
-                nc.sync.dma_start(out=out_v[:, t, (k_ch - 1) * CH:(k_ch + 1) * CH], in_=res[:])
+        def expo(t, h):
+            res = rpool.tile([P, UNIT], F32, tag="res", name="res" + str(t) + "_" + str(h))
+            nc.scalar.activation(out=res[:], in_=args[(t, h)][:], func=ACT.Exp, bias=lnv[:, 0:1])
+            nc.sync.dma_start(out=out_v[:, t, h * UNIT:(h + 1) * UNIT], in_=res[:])
 
-        for name, g in (("x", 0), ("x", 1), ("y", 0), ("y", 1)):
-            tpose(name, g, ps_acc, "acc")
-        tpose("y", 2, ps_tr, "tr")
-        tpose("y", 3, ps_wt, "wt")
-        tpose("y", 4, ps_wt, "wt")
+        order = (
+            ("y", 0), ("y", 1), ("y", 2), ("y", 3), ("x", 0), ("x", 1), ("x", 2), ("x", 3),
+            ("x", 4), ("x", 5), ("x", 6), ("x", 7), ("y", 4), ("y", 5), ("y", 6), ("y", 7),
+        )
+        for i in range(4):
+            tpose(order[i][0], order[i][1])
 
         x5 = const.tile([P, 5], F32)
         nc.vector.tensor_copy(out=x5[:, 0:4], in_=lraw[:])
@@ -251,7 +197,8 @@ def tile_rbf_kernel(tc, X, X2, lengthscale, variance, out):
         lnv = const.tile([P, 1], F32)
         nc.scalar.activation(out=lnv[:], in_=sp[:, 4:5], func=ACT.Ln)
 
-        rlt = ps_wt.tile([P, CH], F32, tag="wt")
+
+        rlt = ps_acc.tile([P, CH], F32, tag="acc")
         for ue in range(4):
             nc.tensor.transpose(
                 out=rlt[:, ue * P:(ue + 1) * P], in_=rl4[:, ue:ue + 1].to_broadcast([P, P]), identity=ident[:]
@@ -261,72 +208,70 @@ def tile_rbf_kernel(tc, X, X2, lengthscale, variance, out):
             out=rlb[:].rearrange("m (u q e) -> m u q e", u=2, e=2),
             in_=rlt[:].rearrange("m (u e q) -> m u q e", u=2, e=2),
         )
-        order = (
-            ("x", 0), ("x", 1), ("y", 0), ("y", 1), ("y", 2), ("y", 3), ("y", 4), ("y", 5),
-            ("y", 6), ("y", 7), ("x", 2), ("x", 3), ("x", 4), ("x", 5), ("x", 6), ("x", 7),
-        )
         for name, g in order:
             rows_scaled(name, g)
 
-        scale("x", 0)
-        scale("x", 1)
-        quant("x", 0)
-        scale("y", 0)
-        quant("x", 1)
-        scale("y", 1)
-        quant("y", 0)
-        scale("y", 2)
-        tpose("y", 6, ps_tr, "tr")
-        quant("y", 1)
-        scale("y", 3)
-        tpose("y", 5, ps_wt, "wt")
-        quant("y", 2)
-        row_norms("x", 0)
-        row_norms("x", 1)
-        scale("y", 4)
-        quant("y", 3)
-        fin_pool("x", 0)
-        spread(0, ps_acc, "acc")
-        scale("y", 5)
-        quant("y", 4)
-        quant("y", 5)
-        row_norms("y", 0)
-        row_norms("y", 1)
-        fin_pool("y", 0)
+        def prep(i):
+            scale(order[i][0], order[i][1])
+            if i + 4 < len(order):
+                tpose(order[i + 4][0], order[i + 4][1])
 
-        plan = {0: (("y", 6), ("y", 7)), 1: (("x", 2),), 2: (("x", 3),), 3: (("x", 4),), 4: (("x", 5),), 5: (("x", 6),), 6: (("x", 7),)}
-        norms_at = {
-            0: (("y", 2), ("y", 3)), 1: (("y", 4), ("y", 5)), 2: (("y", 6), ("y", 7)), 3: (("x", 2), ("x", 3)),
-            4: (("x", 4), ("x", 5)), 5: (("x", 6),), 6: (("x", 7),),
-        }
-        steps = NCH * NCH
-        for s in range(steps + 1):
-            cur = plan.get(s, ())
-            nxt = plan.get(s + 1, ())
-            if s in (1, 2, 3):
-                fin_pool("y", s)
-            if s in (4, 7, 11):
-                fin_pool("x", (s + 1) // 4)
-                spread((s + 1) // 4, ps_wt, "wt")
-            if s < steps:
-                mx(s)
-            if len(cur) > 0:
-                scale(cur[0][0], cur[0][1])
-            if len(cur) > 1:
-                tpose(cur[1][0], cur[1][1], ps_tr, "tr")
-            if s < steps:
-                stt(s, (0, 1))
-            if len(cur) > 1:
-                scale(cur[1][0], cur[1][1])
-            if s > 0:
-                for tl in range(4):
-                    tp4(s - 1, tl)
-                    expo(s - 1, tl)
-            for name, g in norms_at.get(s, ()):
-                row_norms(name, g)
-            if len(nxt) > 0:
-                tpose(nxt[0][0], nxt[0][1], ps_tr, "tr")
-            if s < steps:
-                stt(s, (2, 3))
-            for name, g in cur:
-                quant(name, g)
+        def qnt(i):
+            quant(order[i][0], order[i][1])
+
+        def rn(i):
+            row_norms(order[i][0], order[i][1])
+
+        prep(0)
+        for i in range(1, 10):
+            prep(i)
+            qnt(i - 1)
+            if i <= 4:
+                rn(i - 1)
+        fetch(0, 8)
+        spread(0, ps_acc, "acc")
+        spread(1, ps_acc, "acc")
+        rn(4)
+        rn(5)
+        prep(10)
+        qnt(9)
+        prep(11)
+        qnt(10)
+        qnt(11)
+
+        units = [(t, 0) for t in range(TILES)] + [(t, 1) for t in range(TILES)]
+
+        def on_pool(u):
+            return u in (12, 14) or (u >= TILES and u % 2 == 0)
+
+        def unit(u):
+            addu(units[u][0], units[u][1], on_pool(u))
+            if u >= 1 and not on_pool(u - 1):
+                clamp(units[u - 1][0], units[u - 1][1])
+            if u >= LAG:
+                expo(units[u - LAG][0], units[u - LAG][1])
+
+        norms_after = {2: (6,), 3: (7,), 5: (8,), 6: (9,), 7: (10,), 9: (11,), 10: (12,), 11: (13,), 12: (14, 15)}
+        prep_after = {1: 12, 4: 13, 7: 14, 10: 15}
+        for u in range(len(units)):
+            t, h = units[u]
+            if u == 14:
+                fetch(8, 8)
+                spread(2, ps_tr, "tr")
+                spread(3, ps_tr, "tr")
+            if u % 2 == 0:
+                mxu(t, h)
+                mxu(t + 1, h)
+                if h == 0:
+                    fetch(TILES + t, 2)
+            unit(u)
+            for i in norms_after.get(u, ()):
+                rn(i)
+            if u in prep_after:
+                prep(prep_after[u])
+            if u - 1 in prep_after:
+                qnt(prep_after[u - 1])
+        last = len(units) - 1
+        clamp(units[last][0], units[last][1])
+        for u in range(last - LAG + 1, last + 1):
+            expo(units[u][0], units[u][1])

@@ -31,7 +31,9 @@ def tile_rbf_kernel(tc, X, X2, lengthscale, variance, out):
         apool = ctx.enter_context(tc.tile_pool(name="apool", bufs=8))
         rpool = ctx.enter_context(tc.tile_pool(name="rpool", bufs=4))
         ps_acc = ctx.enter_context(tc.psum_pool(name="ps_acc", bufs=4))
-        ps_tr = ctx.enter_context(tc.psum_pool(name="ps_tr", bufs=4))
+        ps_tr = ctx.enter_context(tc.psum_pool(name="ps_tr", bufs=2))
+        ps_n = ctx.enter_context(tc.psum_pool(name="ps_n", bufs=1))
+        ps_m = ctx.enter_context(tc.psum_pool(name="ps_m", bufs=1))
 
         lraw = const.tile([P, 4], BF16)
         vraw = const.tile([P, 1], BF16)
@@ -47,7 +49,7 @@ def tile_rbf_kernel(tc, X, X2, lengthscale, variance, out):
         out_v = out.rearrange("(t p) j -> p t j", p=P)
         for raw, view, lo in (
             (x2_raw, x2_v, 0), (x2_raw, x2_v, 4), (x_raw, x_v, 0), (x_raw, x_v, 4),
-            (x_raw, x_v, 8), (x_raw, x_v, 12), (x2_raw, x2_v, 8), (x2_raw, x2_v, 12),
+            (x2_raw, x2_v, 8), (x_raw, x_v, 8), (x_raw, x_v, 12), (x2_raw, x2_v, 12),
         ):
             nc.sync.dma_start(out=raw[:, lo:lo + 4, :], in_=view[:, lo:lo + 4, :])
         raws = {"x": x_raw, "y": x2_raw}
@@ -60,14 +62,13 @@ def tile_rbf_kernel(tc, X, X2, lengthscale, variance, out):
         for name in ("x", "y"):
             codes[name] = const.tile([P, ROWS], U32, name="codes_" + name, align_bytes=64)
             scls[name] = const.tile([P, ROWS], U8, name="scls_" + name, align_bytes=64)
-        ncol = {"y": 0, "x": TILES}
-        nsum = const.tile([P, 2 * TILES], F32)
-        half = const.tile([P, 2 * TILES], F32)
-        junk = const.tile([P, D], BF16)
+        nrm = ps_m.tile([P, TILES], F32)
+        half = const.tile([P, TILES], F32)
         nb = const.tile([P, ROWS], F32)
         grps = {}
         trs = {}
-        u32s = {}
+        sqs = {}
+        nps = {}
 
         def tpose(name, g):
             words = raws[name][:].bitcast(F32)
@@ -91,6 +92,45 @@ def tile_rbf_kernel(tc, X, X2, lengthscale, variance, out):
             )
             grps[(name, g)] = grp
 
+        def square(name, g):
+            sq = stage.tile([P, 4, GCOLS], F32, tag="sq", name="sq_" + name + str(g))
+            nc.scalar.activation(
+                out=sq[:].rearrange("q (u e) r -> q u e r", e=2),
+                in_=trs[(name, g)][:].bitcast(BF16).rearrange("q (u r e) -> q u e r", u=2, e=2),
+                func=ACT.Square,
+            )
+            sqs[(name, g)] = sq
+
+        def colsum(g):
+            acc = ps_n.tile([P, GCOLS], F32, tag="n", name="nps" + str(g))
+            for ue in range(4):
+                nc.tensor.matmul(
+                    out=acc[:],
+                    lhsT=wpos[:, ue:ue + 1].to_broadcast([P, P]),
+                    rhs=sqs[("y", g)][:, ue, :],
+                    start=(ue == 0),
+                    stop=(ue == 3),
+                )
+            nps[g] = acc
+
+        def take(g):
+            nc.scalar.copy(out=nb[:, g * GCOLS:(g + 1) * GCOLS], in_=nps[g][:])
+
+        def matvec(g):
+            for a in range(2):
+                col = 2 * g + a
+                for ue in range(4):
+                    nc.tensor.matmul(
+                        out=nrm[:, col:col + 1],
+                        lhsT=sqs[("x", g)][:, ue, a * P:(a + 1) * P],
+                        rhs=wneg[:, ue:ue + 1],
+                        start=(ue == 0),
+                        stop=(ue == 3),
+                    )
+
+        def fetch(g):
+            nc.vector.tensor_copy(out=half[:, 2 * g:2 * g + 2], in_=nrm[:, 2 * g:2 * g + 2])
+
         def quant(name, g):
             cols = slice(g * GCOLS, (g + 1) * GCOLS)
             nc.vector.quantize_mx(
@@ -98,36 +138,6 @@ def tile_rbf_kernel(tc, X, X2, lengthscale, variance, out):
                 scales=scls[name][:, cols],
                 in_=grps[(name, g)][:],
             )
-
-        def rows_scaled(name, g):
-            u32 = const.tile([P, 2, D], F32, name="u32_" + name + str(g))
-            nc.gpsimd.tensor_tensor(
-                out=u32[:],
-                in0=raws[name][:, 2 * g:2 * g + 2, :],
-                in1=rlb[:].unsqueeze(1).to_broadcast([P, 2, D]),
-                op=ALU.mult,
-            )
-            u32s[(name, g)] = u32
-
-        def row_norms(name, g):
-            for a in range(2):
-                col = ncol[name] + 2 * g + a
-                nc.scalar.activation(
-                    out=junk[:], in_=u32s[(name, g)][:, a, :], func=ACT.Square, accum_out=nsum[:, col:col + 1]
-                )
-
-        def fetch(lo, n):
-            nc.vector.tensor_scalar(out=half[:, lo:lo + n], in0=nsum[:, lo:lo + n], scalar1=-0.5, scalar2=None, op0=ALU.mult)
-
-        def spread(k, pool, tag):
-            sp_ps = pool.tile([P, CH], F32, tag=tag, name="spread" + str(k))
-            for cl in range(4):
-                nc.tensor.transpose(
-                    out=sp_ps[:, cl * P:(cl + 1) * P],
-                    in_=half[:, 4 * k + cl:4 * k + cl + 1].to_broadcast([P, P]),
-                    identity=ident[:],
-                )
-            nc.scalar.mul(out=nb[:, k * CH:(k + 1) * CH], in_=sp_ps[:], mul=-1.0)
 
         accs = {}
         args = {}
@@ -154,7 +164,7 @@ def tile_rbf_kernel(tc, X, X2, lengthscale, variance, out):
                 nc.vector.scalar_tensor_tensor(
                     out=arg[:, kk * CH:(kk + 1) * CH],
                     in0=accs[(t, k)][:],
-                    scalar=half[:, TILES + t:TILES + t + 1],
+                    scalar=half[:, t:t + 1],
                     in1=nb[:, k * CH:(k + 1) * CH],
                     op0=ALU.add,
                     op1=(ALU.min if on_pool else ALU.subtract),
@@ -172,12 +182,13 @@ def tile_rbf_kernel(tc, X, X2, lengthscale, variance, out):
             nc.scalar.activation(out=res[:], in_=args[(t, h)][:], func=ACT.Exp, bias=lnv[:, 0:1])
             nc.sync.dma_start(out=out_v[:, t, h * UNIT:(h + 1) * UNIT], in_=res[:])
 
-        order = (
-            ("y", 0), ("y", 1), ("y", 2), ("y", 3), ("x", 0), ("x", 1), ("x", 2), ("x", 3),
-            ("x", 4), ("x", 5), ("x", 6), ("x", 7), ("y", 4), ("y", 5), ("y", 6), ("y", 7),
+        gseq = (
+            ("y", 0), ("y", 1), ("y", 2), ("y", 3), ("x", 0), ("x", 1), ("x", 2), ("y", 4),
+            ("x", 3), ("x", 4), ("y", 5), ("x", 5), ("x", 6), ("y", 6), ("x", 7), ("y", 7),
         )
-        for i in range(4):
-            tpose(order[i][0], order[i][1])
+        ngr = len(gseq)
+        for i in range(2):
+            tpose(gseq[i][0], gseq[i][1])
 
         x5 = const.tile([P, 5], F32)
         nc.vector.tensor_copy(out=x5[:, 0:4], in_=lraw[:])
@@ -194,55 +205,41 @@ def tile_rbf_kernel(tc, X, X2, lengthscale, variance, out):
         nc.vector.reciprocal(out=rl4[:], in_=sp[:, 0:4])
         wneg = const.tile([P, 4], F32)
         nc.vector.scalar_tensor_tensor(out=wneg[:], in0=rl4[:], scalar=-0.5, in1=rl4[:], op0=ALU.mult, op1=ALU.mult)
+        wpos = const.tile([P, 4], F32)
+        nc.vector.tensor_scalar(out=wpos[:], in0=wneg[:], scalar1=-1.0, scalar2=None, op0=ALU.mult)
+        square("y", 0)
         lnv = const.tile([P, 1], F32)
         nc.scalar.activation(out=lnv[:], in_=sp[:, 4:5], func=ACT.Ln)
 
-
-        rlt = ps_acc.tile([P, CH], F32, tag="acc")
-        for ue in range(4):
-            nc.tensor.transpose(
-                out=rlt[:, ue * P:(ue + 1) * P], in_=rl4[:, ue:ue + 1].to_broadcast([P, P]), identity=ident[:]
-            )
-        rlb = const.tile([P, D], F32)
-        nc.scalar.copy(
-            out=rlb[:].rearrange("m (u q e) -> m u q e", u=2, e=2),
-            in_=rlt[:].rearrange("m (u e q) -> m u q e", u=2, e=2),
-        )
-        for name, g in order:
-            rows_scaled(name, g)
-
         def prep(i):
-            scale(order[i][0], order[i][1])
-            if i + 4 < len(order):
-                tpose(order[i + 4][0], order[i + 4][1])
+            if 0 < i < ngr:
+                square(gseq[i][0], gseq[i][1])
+            if 1 <= i <= ngr and gseq[i - 1][0] == "y":
+                take(gseq[i - 1][1])
+            if i < ngr:
+                scale(gseq[i][0], gseq[i][1])
+                if i + 2 < ngr:
+                    tpose(gseq[i + 2][0], gseq[i + 2][1])
+                if gseq[i][0] == "y":
+                    colsum(gseq[i][1])
+                else:
+                    matvec(gseq[i][1])
 
         def qnt(i):
-            quant(order[i][0], order[i][1])
-
-        def rn(i):
-            row_norms(order[i][0], order[i][1])
+            quant(gseq[i][0], gseq[i][1])
 
         prep(0)
-        for i in range(1, 10):
+        for i in range(1, 6):
             prep(i)
             qnt(i - 1)
-            if i <= 4:
-                rn(i - 1)
-        fetch(0, 8)
-        spread(0, ps_acc, "acc")
-        spread(1, ps_acc, "acc")
-        rn(4)
-        rn(5)
-        prep(10)
-        qnt(9)
-        prep(11)
-        qnt(10)
-        qnt(11)
+        qnt(5)
 
         units = [(t, 0) for t in range(TILES)] + [(t, 1) for t in range(TILES)]
 
         def on_pool(u):
-            return u in (12, 14) or (u >= TILES and u % 2 == 0)
+            if u < TILES:
+                return u % 4 != 3
+            return u % 2 == 0
 
         def unit(u):
             addu(units[u][0], units[u][1], on_pool(u))
@@ -251,26 +248,26 @@ def tile_rbf_kernel(tc, X, X2, lengthscale, variance, out):
             if u >= LAG:
                 expo(units[u - LAG][0], units[u - LAG][1])
 
-        norms_after = {2: (6,), 3: (7,), 5: (8,), 6: (9,), 7: (10,), 9: (11,), 10: (12,), 11: (13,), 12: (14, 15)}
-        prep_after = {1: 12, 4: 13, 7: 14, 10: 15}
-        for u in range(len(units)):
-            t, h = units[u]
-            if u == 14:
-                fetch(8, 8)
-                spread(2, ps_tr, "tr")
-                spread(3, ps_tr, "tr")
-            if u % 2 == 0:
-                mxu(t, h)
-                mxu(t + 1, h)
-                if h == 0:
-                    fetch(TILES + t, 2)
-            unit(u)
-            for i in norms_after.get(u, ()):
-                rn(i)
-            if u in prep_after:
-                prep(prep_after[u])
-            if u - 1 in prep_after:
-                qnt(prep_after[u - 1])
+        nprep = (2, 1, 2, 1, 2, 1, 2, 0)
+        nxt = 6
+        for n in range(8):
+            mxu(2 * n, 0)
+            mxu(2 * n + 1, 0)
+            mine = list(range(nxt, nxt + nprep[n]))
+            nxt += nprep[n]
+            for i in mine:
+                prep(i)
+            fetch(n)
+            unit(2 * n)
+            unit(2 * n + 1)
+            for i in mine:
+                if i < ngr:
+                    qnt(i)
+        for m in range(8):
+            mxu(2 * m, 1)
+            mxu(2 * m + 1, 1)
+            unit(TILES + 2 * m)
+            unit(TILES + 2 * m + 1)
         last = len(units) - 1
         clamp(units[last][0], units[last][1])
         for u in range(last - LAG + 1, last + 1):

@@ -19,21 +19,19 @@ GCOLS = 2 * P
 CH = 512
 UNIT = 2 * CH
 FLOPS = 2 * ROWS * ROWS * D
-LAG = 3
 
 
 def tile_rbf_kernel(tc, X, X2, lengthscale, variance, out):
     nc = tc.nc
     with ExitStack() as ctx:
-        ctx.enter_context(tc.manual_schedule())
         const = ctx.enter_context(tc.tile_pool(name="const", bufs=1))
         stage = ctx.enter_context(tc.tile_pool(name="stage", bufs=3))
-        apool = ctx.enter_context(tc.tile_pool(name="apool", bufs=8))
+        gpool = ctx.enter_context(tc.tile_pool(name="gpool", bufs=13))
+        apool = ctx.enter_context(tc.tile_pool(name="apool", bufs=10))
         rpool = ctx.enter_context(tc.tile_pool(name="rpool", bufs=4))
         ps_acc = ctx.enter_context(tc.psum_pool(name="ps_acc", bufs=4))
-        ps_tr = ctx.enter_context(tc.psum_pool(name="ps_tr", bufs=2))
+        ps_tr = ctx.enter_context(tc.psum_pool(name="ps_tr", bufs=3))
         ps_n = ctx.enter_context(tc.psum_pool(name="ps_n", bufs=1))
-        ps_m = ctx.enter_context(tc.psum_pool(name="ps_m", bufs=1))
 
         lraw = const.tile([P, 4], BF16)
         vraw = const.tile([P, 1], BF16)
@@ -48,8 +46,8 @@ def tile_rbf_kernel(tc, X, X2, lengthscale, variance, out):
         x_v = X.rearrange("(t p) f -> p t f", p=P)
         out_v = out.rearrange("(t p) j -> p t j", p=P)
         for raw, view, lo in (
-            (x2_raw, x2_v, 0), (x2_raw, x2_v, 4), (x_raw, x_v, 0), (x_raw, x_v, 4),
-            (x2_raw, x2_v, 8), (x_raw, x_v, 8), (x_raw, x_v, 12), (x2_raw, x2_v, 12),
+            (x2_raw, x2_v, 0), (x_raw, x_v, 0), (x2_raw, x2_v, 4), (x_raw, x_v, 4),
+            (x_raw, x_v, 8), (x_raw, x_v, 12), (x2_raw, x2_v, 8), (x2_raw, x2_v, 12),
         ):
             nc.sync.dma_start(out=raw[:, lo:lo + 4, :], in_=view[:, lo:lo + 4, :])
         raws = {"x": x_raw, "y": x2_raw}
@@ -62,13 +60,15 @@ def tile_rbf_kernel(tc, X, X2, lengthscale, variance, out):
         for name in ("x", "y"):
             codes[name] = const.tile([P, ROWS], U32, name="codes_" + name, align_bytes=64)
             scls[name] = const.tile([P, ROWS], U8, name="scls_" + name, align_bytes=64)
-        nrm = ps_m.tile([P, TILES], F32)
+        nsum = const.tile([P, TILES], F32)
         half = const.tile([P, TILES], F32)
+        junk = const.tile([P, D], BF16)
         nb = const.tile([P, ROWS], F32)
         grps = {}
         trs = {}
         sqs = {}
         nps = {}
+        u32s = {}
 
         def tpose(name, g):
             words = raws[name][:].bitcast(F32)
@@ -83,7 +83,7 @@ def tile_rbf_kernel(tc, X, X2, lengthscale, variance, out):
             trs[(name, g)] = tr
 
         def scale(name, g):
-            grp = stage.tile([P, 4 * GCOLS], BF16, tag="grp", name="grp_" + name + str(g), align_bytes=64)
+            grp = gpool.tile([P, 4 * GCOLS], BF16, tag="grp", name="grp_" + name + str(g), align_bytes=64)
             nc.vector.tensor_tensor(
                 out=grp[:].rearrange("q (r u e) -> q r u e", u=2, e=2),
                 in0=trs[(name, g)][:].bitcast(BF16).rearrange("q (u r e) -> q r u e", u=2, e=2),
@@ -116,20 +116,16 @@ def tile_rbf_kernel(tc, X, X2, lengthscale, variance, out):
         def take(g):
             nc.scalar.copy(out=nb[:, g * GCOLS:(g + 1) * GCOLS], in_=nps[g][:])
 
-        def matvec(g):
-            for a in range(2):
-                col = 2 * g + a
-                for ue in range(4):
-                    nc.tensor.matmul(
-                        out=nrm[:, col:col + 1],
-                        lhsT=sqs[("x", g)][:, ue, a * P:(a + 1) * P],
-                        rhs=wneg[:, ue:ue + 1],
-                        start=(ue == 0),
-                        stop=(ue == 3),
-                    )
+        def rows_scaled(t):
+            u32 = const.tile([P, D], F32, name="u32_" + str(t))
+            nc.gpsimd.tensor_tensor(out=u32[:], in0=x_raw[:, t, :], in1=rlb[:], op=ALU.mult)
+            u32s[t] = u32
 
-        def fetch(g):
-            nc.vector.tensor_copy(out=half[:, 2 * g:2 * g + 2], in_=nrm[:, 2 * g:2 * g + 2])
+        def row_norm(t):
+            nc.scalar.activation(out=junk[:], in_=u32s[t][:], func=ACT.Square, accum_out=nsum[:, t:t + 1])
+
+        def fetch(lo, n):
+            nc.vector.tensor_scalar(out=half[:, lo:lo + n], in0=nsum[:, lo:lo + n], scalar1=-0.5, scalar2=None, op0=ALU.mult)
 
         def quant(name, g):
             cols = slice(g * GCOLS, (g + 1) * GCOLS)
@@ -157,7 +153,7 @@ def tile_rbf_kernel(tc, X, X2, lengthscale, variance, out):
                 )
                 accs[(t, k)] = acc
 
-        def addu(t, h, on_pool):
+        def addu(t, h):
             arg = apool.tile([P, UNIT], F32, tag="arg", name="arg" + str(t) + "_" + str(h))
             for kk in range(2):
                 k = 2 * h + kk
@@ -167,28 +163,31 @@ def tile_rbf_kernel(tc, X, X2, lengthscale, variance, out):
                     scalar=half[:, t:t + 1],
                     in1=nb[:, k * CH:(k + 1) * CH],
                     op0=ALU.add,
-                    op1=(ALU.min if on_pool else ALU.subtract),
+                    op1=ALU.subtract,
                 )
             args[(t, h)] = arg
-            if on_pool:
-                nc.gpsimd.tensor_tensor(out=arg[:], in0=arg[:], in1=nb[:, h * UNIT:(h + 1) * UNIT], op=ALU.subtract)
 
         def clamp(t, h):
             arg = args[(t, h)]
             nc.vector.tensor_scalar(out=arg[:], in0=arg[:], scalar1=0.0, scalar2=None, op0=ALU.min)
 
-        def expo(t, h):
+        def expo(t, h, clamped):
+            arg = args[(t, h)]
             res = rpool.tile([P, UNIT], F32, tag="res", name="res" + str(t) + "_" + str(h))
-            nc.scalar.activation(out=res[:], in_=args[(t, h)][:], func=ACT.Exp, bias=lnv[:, 0:1])
+            if clamped:
+                nc.scalar.activation(out=res[:], in_=arg[:], func=ACT.Exp, bias=lnv[:, 0:1])
+            else:
+                nc.scalar.activation(out=arg[:], in_=arg[:], func=ACT.Relu, scale=-1.0)
+                nc.scalar.activation(out=res[:], in_=arg[:], func=ACT.Exp, bias=lnv[:, 0:1], scale=-1.0)
             nc.sync.dma_start(out=out_v[:, t, h * UNIT:(h + 1) * UNIT], in_=res[:])
 
-        gseq = (
-            ("y", 0), ("y", 1), ("y", 2), ("y", 3), ("x", 0), ("x", 1), ("x", 2), ("y", 4),
-            ("x", 3), ("x", 4), ("y", 5), ("x", 5), ("x", 6), ("y", 6), ("x", 7), ("y", 7),
+        order = (
+            ("y", 0), ("x", 0), ("y", 1), ("x", 1), ("y", 2), ("x", 2), ("y", 3), ("x", 3),
+            ("x", 4), ("x", 5), ("x", 6), ("x", 7), ("y", 4), ("y", 5), ("y", 6), ("y", 7),
         )
-        ngr = len(gseq)
-        for i in range(2):
-            tpose(gseq[i][0], gseq[i][1])
+        ngr = len(order)
+        for i in range(3):
+            tpose(order[i][0], order[i][1])
 
         x5 = const.tile([P, 5], F32)
         nc.vector.tensor_copy(out=x5[:, 0:4], in_=lraw[:])
@@ -203,72 +202,92 @@ def tile_rbf_kernel(tc, X, X2, lengthscale, variance, out):
         nc.vector.scalar_tensor_tensor(out=sp[:], in0=x5[:], scalar=0.0, in1=lp[:], op0=ALU.max, op1=ALU.add)
         rl4 = const.tile([P, 4], F32)
         nc.vector.reciprocal(out=rl4[:], in_=sp[:, 0:4])
-        wneg = const.tile([P, 4], F32)
-        nc.vector.scalar_tensor_tensor(out=wneg[:], in0=rl4[:], scalar=-0.5, in1=rl4[:], op0=ALU.mult, op1=ALU.mult)
         wpos = const.tile([P, 4], F32)
-        nc.vector.tensor_scalar(out=wpos[:], in0=wneg[:], scalar1=-1.0, scalar2=None, op0=ALU.mult)
+        nc.vector.scalar_tensor_tensor(out=wpos[:], in0=rl4[:], scalar=0.5, in1=rl4[:], op0=ALU.mult, op1=ALU.mult)
         square("y", 0)
         lnv = const.tile([P, 1], F32)
         nc.scalar.activation(out=lnv[:], in_=sp[:, 4:5], func=ACT.Ln)
 
-        def prep(i):
-            if 0 < i < ngr:
-                square(gseq[i][0], gseq[i][1])
-            if 1 <= i <= ngr and gseq[i - 1][0] == "y":
-                take(gseq[i - 1][1])
-            if i < ngr:
-                scale(gseq[i][0], gseq[i][1])
-                if i + 2 < ngr:
-                    tpose(gseq[i + 2][0], gseq[i + 2][1])
-                if gseq[i][0] == "y":
-                    colsum(gseq[i][1])
-                else:
-                    matvec(gseq[i][1])
 
-        def qnt(i):
-            quant(gseq[i][0], gseq[i][1])
+        rlt = ps_acc.tile([P, CH], F32, tag="acc")
+        for ue in range(4):
+            nc.tensor.transpose(
+                out=rlt[:, ue * P:(ue + 1) * P], in_=rl4[:, ue:ue + 1].to_broadcast([P, P]), identity=ident[:]
+            )
+        rlb = const.tile([P, D], F32)
+        nc.scalar.copy(
+            out=rlb[:].rearrange("m (u q e) -> m u q e", u=2, e=2),
+            in_=rlt[:].rearrange("m (u e q) -> m u q e", u=2, e=2),
+        )
+        for t in range(TILES):
+            rows_scaled(t)
 
-        prep(0)
-        for i in range(1, 6):
-            prep(i)
-            qnt(i - 1)
-        qnt(5)
+        def prep_a(i):
+            name, g = order[i]
+            if name == "y" and i > 0:
+                square(name, g)
+            scale(name, g)
+            if i + 3 < ngr:
+                tpose(order[i + 3][0], order[i + 3][1])
+
+        def prep_b(i):
+            name, g = order[i]
+            if name == "y":
+                if g > 0:
+                    take(g - 1)
+                colsum(g)
+            else:
+                row_norm(2 * g)
+                row_norm(2 * g + 1)
+
+        for i in range(12):
+            prep_a(i)
+            prep_b(i)
+        take(3)
+        for i in range(12):
+            quant(order[i][0], order[i][1])
+        fetch(0, 8)
 
         units = [(t, 0) for t in range(TILES)] + [(t, 1) for t in range(TILES)]
+        nun = len(units)
 
-        def on_pool(u):
-            if u < TILES:
-                return u % 4 != 3
-            return u % 2 == 0
+        def by_vector(u):
+            return u % 4 != 3 or u >= nun - 4
 
-        def unit(u):
-            addu(units[u][0], units[u][1], on_pool(u))
-            if u >= 1 and not on_pool(u - 1):
-                clamp(units[u - 1][0], units[u - 1][1])
-            if u >= LAG:
-                expo(units[u - LAG][0], units[u - LAG][1])
+        def clamps(us):
+            for w in us:
+                if by_vector(w):
+                    clamp(units[w][0], units[w][1])
 
-        nprep = (2, 1, 2, 1, 2, 1, 2, 0)
-        nxt = 6
-        for n in range(8):
-            mxu(2 * n, 0)
-            mxu(2 * n + 1, 0)
-            mine = list(range(nxt, nxt + nprep[n]))
-            nxt += nprep[n]
-            for i in mine:
-                prep(i)
-            fetch(n)
-            unit(2 * n)
-            unit(2 * n + 1)
-            for i in mine:
-                if i < ngr:
-                    qnt(i)
-        for m in range(8):
-            mxu(2 * m, 1)
-            mxu(2 * m + 1, 1)
-            unit(TILES + 2 * m)
-            unit(TILES + 2 * m + 1)
-        last = len(units) - 1
-        clamp(units[last][0], units[last][1])
-        for u in range(last - LAG + 1, last + 1):
-            expo(units[u][0], units[u][1])
+        def exps(us):
+            for w in us:
+                expo(units[w][0], units[w][1], by_vector(w))
+
+        late_a = {0: 12, 3: 13, 6: 14, 9: 15}
+        late_b = {1: 12, 4: 13, 7: 14, 10: 15}
+        mxu(units[0][0], units[0][1])
+        mxu(units[1][0], units[1][1])
+        for u in range(nun):
+            if u in late_a:
+                prep_a(late_a[u])
+            addu(units[u][0], units[u][1])
+            if u + 2 < nun:
+                mxu(units[u + 2][0], units[u + 2][1])
+            if u in late_b and late_b[u] > 12:
+                prep_b(late_b[u])
+            if u in late_b and late_b[u] == 12:
+                colsum(4)
+            if u == nun - 3:
+                clamps((u - 1, u))
+            if u % 4 == 1 and u >= 5:
+                exps(range(u - 5, u - 1))
+            if u % 4 == 3 and u < nun - 4:
+                clamps(range(u - 3, u + 1))
+            if u == 7:
+                fetch(8, 8)
+            if u == 11:
+                take(7)
+                for i in range(12, ngr):
+                    quant(order[i][0], order[i][1])
+        clamps((nun - 2, nun - 1))
+        exps(range(nun - 4, nun))

@@ -169,16 +169,16 @@ def tile_rbf_kernel(tc, X, X2, lengthscale, variance, out):
 
         def clamp(t, h):
             arg = args[(t, h)]
+            nc.gpsimd.tensor_scalar(out=arg[:], in0=arg[:], scalar1=0.0, scalar2=-1.0e30, op0=ALU.min, op1=ALU.max)
+
+        def clamp_v(t, h):
+            arg = args[(t, h)]
             nc.vector.tensor_scalar(out=arg[:], in0=arg[:], scalar1=0.0, scalar2=None, op0=ALU.min)
 
-        def expo(t, h, clamped):
+        def expo(t, h):
             arg = args[(t, h)]
             res = rpool.tile([P, UNIT], F32, tag="res", name="res" + str(t) + "_" + str(h))
-            if clamped:
-                nc.scalar.activation(out=res[:], in_=arg[:], func=ACT.Exp, bias=lnv[:, 0:1])
-            else:
-                nc.scalar.activation(out=arg[:], in_=arg[:], func=ACT.Relu, scale=-1.0)
-                nc.scalar.activation(out=res[:], in_=arg[:], func=ACT.Exp, bias=lnv[:, 0:1], scale=-1.0)
+            nc.scalar.activation(out=res[:], in_=arg[:], func=ACT.Exp, bias=lnv[:, 0:1])
             nc.sync.dma_start(out=out_v[:, t, h * UNIT:(h + 1) * UNIT], in_=res[:])
 
         order = (
@@ -251,18 +251,6 @@ def tile_rbf_kernel(tc, X, X2, lengthscale, variance, out):
         units = [(t, 0) for t in range(TILES)] + [(t, 1) for t in range(TILES)]
         nun = len(units)
 
-        def by_vector(u):
-            return u % 4 != 3 or u >= nun - 4
-
-        def clamps(us):
-            for w in us:
-                if by_vector(w):
-                    clamp(units[w][0], units[w][1])
-
-        def exps(us):
-            for w in us:
-                expo(units[w][0], units[w][1], by_vector(w))
-
         late_a = {0: 12, 3: 13, 6: 14, 9: 15}
         late_b = {1: 12, 4: 13, 7: 14, 10: 15}
         mxu(units[0][0], units[0][1])
@@ -277,17 +265,17 @@ def tile_rbf_kernel(tc, X, X2, lengthscale, variance, out):
                 prep_b(late_b[u])
             if u in late_b and late_b[u] == 12:
                 colsum(4)
-            if u == nun - 3:
-                clamps((u - 1, u))
-            if u % 4 == 1 and u >= 5:
-                exps(range(u - 5, u - 1))
-            if u % 4 == 3 and u < nun - 4:
-                clamps(range(u - 3, u + 1))
+            if u < nun - 3:
+                clamp(units[u][0], units[u][1])
+            else:
+                clamp_v(units[u][0], units[u][1])
+            if u >= 2:
+                expo(units[u - 2][0], units[u - 2][1])
             if u == 7:
                 fetch(8, 8)
             if u == 11:
                 take(7)
                 for i in range(12, ngr):
                     quant(order[i][0], order[i][1])
-        clamps((nun - 2, nun - 1))
-        exps(range(nun - 4, nun))
+        for u in range(nun - 2, nun):
+            expo(units[u][0], units[u][1])

@@ -1,3 +1,4 @@
+import math
 from contextlib import ExitStack
 
 import concourse.mybir as mybir
@@ -10,6 +11,7 @@ U8 = mybir.dt.uint8
 FP8X4 = mybir.dt.float8_e4m3fn_x4
 ALU = mybir.AluOpType
 ACT = mybir.ActivationFunctionType
+ENG = mybir.EngineType
 
 P = 128
 ROWS = 2048
@@ -25,13 +27,13 @@ def tile_rbf_kernel(tc, X, X2, lengthscale, variance, out):
     nc = tc.nc
     with ExitStack() as ctx:
         const = ctx.enter_context(tc.tile_pool(name="const", bufs=1))
-        stage = ctx.enter_context(tc.tile_pool(name="stage", bufs=3))
-        gpool = ctx.enter_context(tc.tile_pool(name="gpool", bufs=13))
+        stage = ctx.enter_context(tc.tile_pool(name="stage", bufs=4))
+        upool = ctx.enter_context(tc.tile_pool(name="upool", bufs=8))
+        gpool = ctx.enter_context(tc.tile_pool(name="gpool", bufs=16))
         apool = ctx.enter_context(tc.tile_pool(name="apool", bufs=10))
-        rpool = ctx.enter_context(tc.tile_pool(name="rpool", bufs=4))
+        rpool = ctx.enter_context(tc.tile_pool(name="rpool", bufs=5))
         ps_acc = ctx.enter_context(tc.psum_pool(name="ps_acc", bufs=4))
-        ps_tr = ctx.enter_context(tc.psum_pool(name="ps_tr", bufs=3))
-        ps_n = ctx.enter_context(tc.psum_pool(name="ps_n", bufs=1))
+        ps_tr = ctx.enter_context(tc.psum_pool(name="ps_tr", bufs=4))
 
         lraw = const.tile([P, 4], BF16)
         vraw = const.tile([P, 1], BF16)
@@ -39,17 +41,18 @@ def tile_rbf_kernel(tc, X, X2, lengthscale, variance, out):
             out=lraw[:].rearrange("q (u e) -> q u e", e=2),
             in_=lengthscale.rearrange("o (u q e) -> (o q) u e", u=2, e=2),
         )
-        nc.sync.dma_start(out=vraw[:], in_=variance.partition_broadcast(P))
         x2_raw = const.tile([P, TILES, D], BF16)
         x_raw = const.tile([P, TILES, D], BF16)
         x2_v = X2.rearrange("(c p) f -> p c f", p=P)
         x_v = X.rearrange("(t p) f -> p t f", p=P)
         out_v = out.rearrange("(t p) j -> p t j", p=P)
-        for raw, view, lo in (
-            (x2_raw, x2_v, 0), (x_raw, x_v, 0), (x2_raw, x2_v, 4), (x_raw, x_v, 4),
-            (x_raw, x_v, 8), (x_raw, x_v, 12), (x2_raw, x2_v, 8), (x2_raw, x2_v, 12),
+        for raw, view, lo, hi in (
+            (x2_raw, x2_v, 0, 2), (x_raw, x_v, 0, 2), (x2_raw, x2_v, 2, 4), (x_raw, x_v, 2, 4),
+            (x2_raw, x2_v, 4, 8), (x_raw, x_v, 4, 8),
+            (x_raw, x_v, 8, 12), (x_raw, x_v, 12, 16), (x2_raw, x2_v, 8, 12), (x2_raw, x2_v, 12, 16),
         ):
-            nc.sync.dma_start(out=raw[:, lo:lo + 4, :], in_=view[:, lo:lo + 4, :])
+            nc.sync.dma_start(out=raw[:, lo:hi, :], in_=view[:, lo:hi, :])
+        nc.scalar.dma_start(out=vraw[:], in_=variance.partition_broadcast(P))
         raws = {"x": x_raw, "y": x2_raw}
 
         ident = const.tile([P, P], F32)
@@ -60,8 +63,7 @@ def tile_rbf_kernel(tc, X, X2, lengthscale, variance, out):
         for name in ("x", "y"):
             codes[name] = const.tile([P, ROWS], U32, name="codes_" + name, align_bytes=64)
             scls[name] = const.tile([P, ROWS], U8, name="scls_" + name, align_bytes=64)
-        nsum = const.tile([P, TILES], F32)
-        half = const.tile([P, TILES], F32)
+        xn2 = const.tile([P, TILES], F32)
         junk = const.tile([P, D], BF16)
         nb = const.tile([P, ROWS], F32)
         grps = {}
@@ -70,7 +72,14 @@ def tile_rbf_kernel(tc, X, X2, lengthscale, variance, out):
         nps = {}
         u32s = {}
 
-        def tpose(name, g):
+        order = (
+            ("y", 0), ("x", 0), ("y", 1), ("x", 1), ("y", 2), ("x", 2), ("y", 3), ("x", 3),
+            ("x", 4), ("x", 5), ("x", 6), ("x", 7), ("y", 4), ("y", 5), ("y", 6), ("y", 7),
+        )
+        ngr = len(order)
+
+        def tpose(i):
+            name, g = order[i]
             words = raws[name][:].bitcast(F32)
             tr = ps_tr.tile([P, 2 * GCOLS], F32, tag="tr", name="tr_" + name + str(g))
             for a in range(2):
@@ -80,65 +89,72 @@ def tile_rbf_kernel(tc, X, X2, lengthscale, variance, out):
                         in_=words[:, 2 * g + a, u * P:(u + 1) * P],
                         identity=ident[:],
                     )
-            trs[(name, g)] = tr
+            trs[i] = tr
 
-        def scale(name, g):
+        def scale(i):
+            name, g = order[i]
             grp = gpool.tile([P, 4 * GCOLS], BF16, tag="grp", name="grp_" + name + str(g), align_bytes=64)
             nc.vector.tensor_tensor(
                 out=grp[:].rearrange("q (r u e) -> q r u e", u=2, e=2),
-                in0=trs[(name, g)][:].bitcast(BF16).rearrange("q (u r e) -> q r u e", u=2, e=2),
+                in0=trs[i][:].bitcast(BF16).rearrange("q (u r e) -> q r u e", u=2, e=2),
                 in1=rl4[:].rearrange("q (u e) -> q u e", e=2).unsqueeze(1).to_broadcast([P, GCOLS, 2, 2]),
                 op=ALU.mult,
             )
-            grps[(name, g)] = grp
+            grps[i] = grp
 
-        def square(name, g):
+        def square(i):
+            name, g = order[i]
             sq = stage.tile([P, 4, GCOLS], F32, tag="sq", name="sq_" + name + str(g))
             nc.scalar.activation(
                 out=sq[:].rearrange("q (u e) r -> q u e r", e=2),
-                in_=trs[(name, g)][:].bitcast(BF16).rearrange("q (u r e) -> q u e r", u=2, e=2),
+                in_=trs[i][:].bitcast(BF16).rearrange("q (u r e) -> q u e r", u=2, e=2),
                 func=ACT.Square,
             )
-            sqs[(name, g)] = sq
+            sqs[g] = sq
 
         def colsum(g):
-            acc = ps_n.tile([P, GCOLS], F32, tag="n", name="nps" + str(g))
+            if g % 2 == 0:
+                acc = ps_acc.tile([P, CH], F32, tag="acc", name="nps" + str(g))
+                nps[g // 2] = acc
+            acc = nps[g // 2]
             for ue in range(4):
                 nc.tensor.matmul(
-                    out=acc[:],
+                    out=acc[:, (g % 2) * GCOLS:(g % 2 + 1) * GCOLS],
                     lhsT=wpos[:, ue:ue + 1].to_broadcast([P, P]),
-                    rhs=sqs[("y", g)][:, ue, :],
+                    rhs=sqs[g][:, ue, :],
                     start=(ue == 0),
                     stop=(ue == 3),
                 )
-            nps[g] = acc
 
-        def take(g):
-            nc.scalar.copy(out=nb[:, g * GCOLS:(g + 1) * GCOLS], in_=nps[g][:])
+        def take(k):
+            nc.scalar.copy(out=nb[:, k * CH:(k + 1) * CH], in_=nps[k][:])
 
         def rows_scaled(t):
-            u32 = const.tile([P, D], F32, name="u32_" + str(t))
+            u32 = upool.tile([P, D], F32, tag="u32", name="u32_" + str(t))
             nc.gpsimd.tensor_tensor(out=u32[:], in0=x_raw[:, t, :], in1=rlb[:], op=ALU.mult)
             u32s[t] = u32
 
         def row_norm(t):
-            nc.scalar.activation(out=junk[:], in_=u32s[t][:], func=ACT.Square, accum_out=nsum[:, t:t + 1])
+            nc.scalar.activation(
+                out=junk[:], in_=u32s[t][:], func=ACT.Square, scale=math.sqrt(0.5), accum_out=xn2[:, t:t + 1]
+            )
 
-        def fetch(lo, n):
-            nc.vector.tensor_scalar(out=half[:, lo:lo + n], in0=nsum[:, lo:lo + n], scalar1=-0.5, scalar2=None, op0=ALU.mult)
-
-        def quant(name, g):
+        def quant(i):
+            name, g = order[i]
             cols = slice(g * GCOLS, (g + 1) * GCOLS)
             nc.vector.quantize_mx(
                 out=codes[name][:, cols].bitcast(FP8X4),
                 scales=scls[name][:, cols],
-                in_=grps[(name, g)][:],
+                in_=grps[i][:],
             )
 
         accs = {}
         args = {}
+        units = [(t, 0) for t in range(TILES)] + [(t, 1) for t in range(TILES)]
+        nun = len(units)
 
-        def mxu(t, h):
+        def mxu(w):
+            t, h = units[w]
             for kk in range(2):
                 k = 2 * h + kk
                 acc = ps_acc.tile([P, CH], F32, tag="acc", name="acc" + str(t) + "_" + str(k))
@@ -153,61 +169,61 @@ def tile_rbf_kernel(tc, X, X2, lengthscale, variance, out):
                 )
                 accs[(t, k)] = acc
 
-        def addu(t, h):
+        def addu(w):
+            t, h = units[w]
             arg = apool.tile([P, UNIT], F32, tag="arg", name="arg" + str(t) + "_" + str(h))
             for kk in range(2):
                 k = 2 * h + kk
                 nc.vector.scalar_tensor_tensor(
                     out=arg[:, kk * CH:(kk + 1) * CH],
                     in0=accs[(t, k)][:],
-                    scalar=half[:, t:t + 1],
+                    scalar=xn2[:, t:t + 1],
                     in1=nb[:, k * CH:(k + 1) * CH],
-                    op0=ALU.add,
+                    op0=ALU.subtract,
                     op1=ALU.subtract,
                 )
-            args[(t, h)] = arg
+            args[w] = arg
 
-        def clamp(t, h):
-            arg = args[(t, h)]
+        def clamp(w):
+            arg = args[w]
             nc.gpsimd.tensor_scalar(out=arg[:], in0=arg[:], scalar1=0.0, scalar2=-1.0e30, op0=ALU.min, op1=ALU.max)
 
-        def clamp_v(t, h):
-            arg = args[(t, h)]
+        def clamp_v(w):
+            arg = args[w]
             nc.vector.tensor_scalar(out=arg[:], in0=arg[:], scalar1=0.0, scalar2=None, op0=ALU.min)
 
-        def expo(t, h):
-            arg = args[(t, h)]
+        def expo(w):
+            t, h = units[w]
+            arg = args[w]
             res = rpool.tile([P, UNIT], F32, tag="res", name="res" + str(t) + "_" + str(h))
             nc.scalar.activation(out=res[:], in_=arg[:], func=ACT.Exp, bias=lnv[:, 0:1])
             nc.sync.dma_start(out=out_v[:, t, h * UNIT:(h + 1) * UNIT], in_=res[:])
 
-        order = (
-            ("y", 0), ("x", 0), ("y", 1), ("x", 1), ("y", 2), ("x", 2), ("y", 3), ("x", 3),
-            ("x", 4), ("x", 5), ("x", 6), ("x", 7), ("y", 4), ("y", 5), ("y", 6), ("y", 7),
-        )
-        ngr = len(order)
-        for i in range(3):
-            tpose(order[i][0], order[i][1])
+        pins = tc.manual_schedule(engines={ENG.PE, ENG.DVE, ENG.Activation, ENG.Pool})
+        ctx.enter_context(pins)
 
-        x5 = const.tile([P, 5], F32)
-        nc.vector.tensor_copy(out=x5[:, 0:4], in_=lraw[:])
-        nc.vector.tensor_copy(out=x5[:, 4:5], in_=vraw[:])
-        ax = const.tile([P, 5], F32)
-        nc.scalar.activation(out=ax[:], in_=x5[:], func=ACT.Abs)
-        ex = const.tile([P, 5], F32)
-        nc.scalar.activation(out=ex[:], in_=ax[:], func=ACT.Exp, scale=-1.0)
-        lp = const.tile([P, 5], F32)
+        for i in range(4):
+            tpose(i)
+
+        one = const.tile([P, 4], F32)
+        nc.vector.memset(one[:], 1.0)
+        warm = const.tile([P, 4], F32)
+        nc.scalar.activation(out=warm[:], in_=one[:], func=ACT.Ln)
+        base = const.tile([P, 4], F32)
+        nc.gpsimd.tensor_scalar(out=base[:], in0=one[:], scalar1=math.e, scalar2=None, op0=ALU.mult)
+        nl = const.tile([P, 4], F32)
+        nc.vector.scalar_tensor_tensor(out=nl[:], in0=lraw[:], scalar=-1.0, in1=lraw[:], op0=ALU.mult, op1=ALU.min)
+        ex = const.tile([P, 4], F32)
+        nc.gpsimd.tensor_tensor(out=ex[:], in0=base[:], in1=nl[:], op=ALU.pow)
+        lp = const.tile([P, 4], F32)
         nc.scalar.activation(out=lp[:], in_=ex[:], func=ACT.Ln, bias=1.0)
-        sp = const.tile([P, 5], F32)
-        nc.vector.scalar_tensor_tensor(out=sp[:], in0=x5[:], scalar=0.0, in1=lp[:], op0=ALU.max, op1=ALU.add)
+        sp = const.tile([P, 4], F32)
+        nc.vector.scalar_tensor_tensor(out=sp[:], in0=lraw[:], scalar=0.0, in1=lp[:], op0=ALU.max, op1=ALU.add)
         rl4 = const.tile([P, 4], F32)
-        nc.vector.reciprocal(out=rl4[:], in_=sp[:, 0:4])
+        nc.vector.reciprocal(out=rl4[:], in_=sp[:])
+        scale(0)
         wpos = const.tile([P, 4], F32)
         nc.vector.scalar_tensor_tensor(out=wpos[:], in0=rl4[:], scalar=0.5, in1=rl4[:], op0=ALU.mult, op1=ALU.mult)
-        square("y", 0)
-        lnv = const.tile([P, 1], F32)
-        nc.scalar.activation(out=lnv[:], in_=sp[:, 4:5], func=ACT.Ln)
-
 
         rlt = ps_acc.tile([P, CH], F32, tag="acc")
         for ue in range(4):
@@ -219,63 +235,71 @@ def tile_rbf_kernel(tc, X, X2, lengthscale, variance, out):
             out=rlb[:].rearrange("m (u q e) -> m u q e", u=2, e=2),
             in_=rlt[:].rearrange("m (u e q) -> m u q e", u=2, e=2),
         )
-        for t in range(TILES):
+        nv = const.tile([P, 1], F32)
+        nc.vector.scalar_tensor_tensor(out=nv[:], in0=vraw[:], scalar=-1.0, in1=vraw[:], op0=ALU.mult, op1=ALU.min)
+        ev = const.tile([P, 1], F32)
+        nc.gpsimd.tensor_tensor(out=ev[:], in0=base[:, 0:1], in1=nv[:], op=ALU.pow)
+        lv = const.tile([P, 1], F32)
+        nc.scalar.activation(out=lv[:], in_=ev[:], func=ACT.Ln, bias=1.0)
+        pv = const.tile([P, 1], F32)
+        nc.scalar.activation(out=pv[:], in_=vraw[:], func=ACT.Relu)
+        lnv = const.tile([P, 1], F32)
+        nc.scalar.activation(out=lnv[:], in_=lv[:], func=ACT.Ln, bias=pv[:, 0:1])
+        square(0)
+
+        for t in range(8):
             rows_scaled(t)
+        tpose(4)
+        norms_at = {5: (0, 1), 7: (2, 3), 9: (4, 5), 11: (6, 7)}
+        colsum_at = {4: 0, 6: 1, 8: 2, 10: 3}
+        for i in range(1, 12):
+            scale(i)
+            if order[i][0] == "y":
+                square(i)
+            if i + 4 < ngr:
+                tpose(i + 4)
+            if i in colsum_at:
+                colsum(colsum_at[i])
+            if i in norms_at:
+                for t in norms_at[i]:
+                    row_norm(t)
+            if i == 8:
+                take(0)
+            if i == 11:
+                take(1)
+            if i < 5:
+                rows_scaled(7 + i)
+        for i in (0, 2, 1, 4, 6, 3, 5, 7, 8, 9, 10, 11):
+            quant(i)
 
-        def prep_a(i):
-            name, g = order[i]
-            if name == "y" and i > 0:
-                square(name, g)
-            scale(name, g)
-            if i + 3 < ngr:
-                tpose(order[i + 3][0], order[i + 3][1])
-
-        def prep_b(i):
-            name, g = order[i]
-            if name == "y":
-                if g > 0:
-                    take(g - 1)
-                colsum(g)
-            else:
-                row_norm(2 * g)
-                row_norm(2 * g + 1)
-
-        for i in range(12):
-            prep_a(i)
-            prep_b(i)
-        take(3)
-        for i in range(12):
-            quant(order[i][0], order[i][1])
-        fetch(0, 8)
-
-        units = [(t, 0) for t in range(TILES)] + [(t, 1) for t in range(TILES)]
-        nun = len(units)
-
-        late_a = {0: 12, 3: 13, 6: 14, 9: 15}
-        late_b = {1: 12, 4: 13, 7: 14, 10: 15}
-        mxu(units[0][0], units[0][1])
-        mxu(units[1][0], units[1][1])
+        late_scale = {1: 12, 3: 13, 5: 14, 7: 15}
+        mxu(0)
+        mxu(1)
+        for t in range(8, 12):
+            row_norm(t)
         for u in range(nun):
-            if u in late_a:
-                prep_a(late_a[u])
-            addu(units[u][0], units[u][1])
+            addu(u)
             if u + 2 < nun:
-                mxu(units[u + 2][0], units[u + 2][1])
-            if u in late_b and late_b[u] > 12:
-                prep_b(late_b[u])
-            if u in late_b and late_b[u] == 12:
-                colsum(4)
+                mxu(u + 2)
+            if u in late_scale:
+                scale(late_scale[u])
+                square(late_scale[u])
+            if u in (3, 5, 7, 9):
+                colsum(4 + (u - 3) // 2)
+            if u in (7, 11):
+                take(2 + (u - 7) // 4)
             if u < nun - 3:
-                clamp(units[u][0], units[u][1])
+                clamp(u)
             else:
-                clamp_v(units[u][0], units[u][1])
+                clamp_v(u)
+            if u < 4:
+                rows_scaled(12 + u)
             if u >= 2:
-                expo(units[u - 2][0], units[u - 2][1])
-            if u == 7:
-                fetch(8, 8)
-            if u == 11:
-                take(7)
+                expo(u - 2)
+            if 2 <= u < 6:
+                row_norm(10 + u)
+            if u == 9:
                 for i in range(12, ngr):
-                    quant(order[i][0], order[i][1])
+                    quant(i)
         for u in range(nun - 2, nun):
-            expo(units[u][0], units[u][1])
+            expo(u)

@@ -27,13 +27,12 @@ def tile_rbf_kernel(tc, X, X2, lengthscale, variance, out):
     nc = tc.nc
     with ExitStack() as ctx:
         const = ctx.enter_context(tc.tile_pool(name="const", bufs=1))
-        stage = ctx.enter_context(tc.tile_pool(name="stage", bufs=4))
-        upool = ctx.enter_context(tc.tile_pool(name="upool", bufs=8))
-        gpool = ctx.enter_context(tc.tile_pool(name="gpool", bufs=16))
-        apool = ctx.enter_context(tc.tile_pool(name="apool", bufs=10))
-        rpool = ctx.enter_context(tc.tile_pool(name="rpool", bufs=5))
-        ps_acc = ctx.enter_context(tc.psum_pool(name="ps_acc", bufs=4))
-        ps_tr = ctx.enter_context(tc.psum_pool(name="ps_tr", bufs=4))
+        stage = ctx.enter_context(tc.tile_pool(name="stage", bufs=8))
+        upool = ctx.enter_context(tc.tile_pool(name="upool", bufs=5))
+        gpool = ctx.enter_context(tc.tile_pool(name="gpool", bufs=8))
+        apool = ctx.enter_context(tc.tile_pool(name="apool", bufs=5))
+        rpool = ctx.enter_context(tc.tile_pool(name="rpool", bufs=4))
+        psum = ctx.enter_context(tc.psum_pool(name="psum", bufs=8))
 
         lraw = const.tile([P, 4], BF16)
         vraw = const.tile([P, 1], BF16)
@@ -81,7 +80,7 @@ def tile_rbf_kernel(tc, X, X2, lengthscale, variance, out):
         def tpose(i):
             name, g = order[i]
             words = raws[name][:].bitcast(F32)
-            tr = ps_tr.tile([P, 2 * GCOLS], F32, tag="tr", name="tr_" + name + str(g))
+            tr = psum.tile([P, CH], F32, tag="bank", name="tr_" + name + str(g))
             for a in range(2):
                 for u in range(2):
                     nc.tensor.transpose(
@@ -93,14 +92,16 @@ def tile_rbf_kernel(tc, X, X2, lengthscale, variance, out):
 
         def scale(i):
             name, g = order[i]
-            grp = gpool.tile([P, 4 * GCOLS], BF16, tag="grp", name="grp_" + name + str(g), align_bytes=64)
+            if (name, g // 2) not in grps:
+                grp = gpool.tile([P, 8 * GCOLS], BF16, tag="grp", name="grp_" + name + str(g), align_bytes=64)
+                grps[(name, g // 2)] = grp
+            grp = grps[(name, g // 2)]
             nc.vector.tensor_tensor(
-                out=grp[:].rearrange("q (r u e) -> q r u e", u=2, e=2),
+                out=grp[:, (g % 2) * 4 * GCOLS:(g % 2 + 1) * 4 * GCOLS].rearrange("q (r u e) -> q r u e", u=2, e=2),
                 in0=trs[i][:].bitcast(BF16).rearrange("q (u r e) -> q r u e", u=2, e=2),
                 in1=rl4[:].rearrange("q (u e) -> q u e", e=2).unsqueeze(1).to_broadcast([P, GCOLS, 2, 2]),
                 op=ALU.mult,
             )
-            grps[i] = grp
 
         def square(i):
             name, g = order[i]
@@ -112,12 +113,12 @@ def tile_rbf_kernel(tc, X, X2, lengthscale, variance, out):
             )
             sqs[g] = sq
 
-        def colsum(g):
-            if g % 2 == 0:
-                acc = ps_acc.tile([P, CH], F32, tag="acc", name="nps" + str(g))
+        def colsum(g, ues=range(4)):
+            if g % 2 == 0 and 0 in ues:
+                acc = psum.tile([P, CH], F32, tag="bank", name="nps" + str(g))
                 nps[g // 2] = acc
             acc = nps[g // 2]
-            for ue in range(4):
+            for ue in ues:
                 nc.tensor.matmul(
                     out=acc[:, (g % 2) * GCOLS:(g % 2 + 1) * GCOLS],
                     lhsT=wpos[:, ue:ue + 1].to_broadcast([P, P]),
@@ -129,60 +130,65 @@ def tile_rbf_kernel(tc, X, X2, lengthscale, variance, out):
         def take(k):
             nc.scalar.copy(out=nb[:, k * CH:(k + 1) * CH], in_=nps[k][:])
 
-        def rows_scaled(t):
-            u32 = upool.tile([P, D], F32, tag="u32", name="u32_" + str(t))
-            nc.gpsimd.tensor_tensor(out=u32[:], in0=x_raw[:, t, :], in1=rlb[:], op=ALU.mult)
-            u32s[t] = u32
+        def rows_scaled(k):
+            u32 = upool.tile([P, 2, D], F32, tag="u32", name="u32_" + str(k))
+            nc.gpsimd.tensor_tensor(
+                out=u32[:], in0=x_raw[:, 2 * k:2 * k + 2, :], in1=rlb[:].unsqueeze(1).to_broadcast([P, 2, D]), op=ALU.mult
+            )
+            u32s[k] = u32
 
         def row_norm(t):
             nc.scalar.activation(
-                out=junk[:], in_=u32s[t][:], func=ACT.Square, scale=math.sqrt(0.5), accum_out=xn2[:, t:t + 1]
+                out=junk[:], in_=u32s[t // 2][:, t % 2, :], func=ACT.Square, scale=math.sqrt(0.5), accum_out=xn2[:, t:t + 1]
             )
 
-        def quant(i):
-            name, g = order[i]
-            cols = slice(g * GCOLS, (g + 1) * GCOLS)
+        def quant(name, k):
+            cols = slice(k * 2 * GCOLS, (k + 1) * 2 * GCOLS)
             nc.vector.quantize_mx(
                 out=codes[name][:, cols].bitcast(FP8X4),
                 scales=scls[name][:, cols],
-                in_=grps[i][:],
+                in_=grps[(name, k)][:],
             )
 
         accs = {}
         args = {}
-        units = [(t, 0) for t in range(TILES)] + [(t, 1) for t in range(TILES)]
+        units = [(k, h) for h in range(2) for k in range(TILES // 2)]
         nun = len(units)
 
         def mxu(w):
-            t, h = units[w]
-            for kk in range(2):
-                k = 2 * h + kk
-                acc = ps_acc.tile([P, CH], F32, tag="acc", name="acc" + str(t) + "_" + str(k))
-                nc.tensor.matmul_mx(
-                    out=acc[:],
-                    lhsT=codes["x"][:, t * P:(t + 1) * P].bitcast(FP8X4),
-                    lhsT_scale=scls["x"][:, t * P:(t + 1) * P],
-                    rhs=codes["y"][:, k * CH:(k + 1) * CH].bitcast(FP8X4),
-                    rhs_scale=scls["y"][:, k * CH:(k + 1) * CH],
-                    start=True,
-                    stop=True,
-                )
-                accs[(t, k)] = acc
+            k, h = units[w]
+            for a in range(2):
+                for kk in range(2):
+                    t, c = 2 * k + a, 2 * h + kk
+                    acc = psum.tile([P, CH], F32, tag="bank", name="acc" + str(t) + "_" + str(c))
+                    nc.tensor.matmul_mx(
+                        out=acc[:],
+                        lhsT=codes["x"][:, t * P:(t + 1) * P].bitcast(FP8X4),
+                        lhsT_scale=scls["x"][:, t * P:(t + 1) * P],
+                        rhs=codes["y"][:, c * CH:(c + 1) * CH].bitcast(FP8X4),
+                        rhs_scale=scls["y"][:, c * CH:(c + 1) * CH],
+                        start=True,
+                        stop=True,
+                    )
+                    accs[(t, c)] = acc
 
         def addu(w):
-            t, h = units[w]
-            arg = apool.tile([P, UNIT], F32, tag="arg", name="arg" + str(t) + "_" + str(h))
-            for kk in range(2):
-                k = 2 * h + kk
-                nc.vector.scalar_tensor_tensor(
-                    out=arg[:, kk * CH:(kk + 1) * CH],
-                    in0=accs[(t, k)][:],
-                    scalar=xn2[:, t:t + 1],
-                    in1=nb[:, k * CH:(k + 1) * CH],
-                    op0=ALU.subtract,
-                    op1=ALU.subtract,
-                )
+            k, h = units[w]
+            arg = apool.tile([P, 2, UNIT], F32, tag="arg", name="arg" + str(w))
             args[w] = arg
+            for a in range(2):
+                for kk in (1, 0):
+                    t, c = 2 * k + a, 2 * h + kk
+                    nc.vector.scalar_tensor_tensor(
+                        out=arg[:, a, kk * CH:(kk + 1) * CH],
+                        in0=accs[(t, c)][:],
+                        scalar=xn2[:, t:t + 1],
+                        in1=nb[:, c * CH:(c + 1) * CH],
+                        op0=ALU.subtract,
+                        op1=ALU.subtract,
+                    )
+                if w == nun - 1:
+                    nc.vector.tensor_scalar(out=arg[:, a, :], in0=arg[:, a, :], scalar1=0.0, scalar2=None, op0=ALU.min)
 
         def clamp(w):
             arg = args[w]
@@ -193,12 +199,22 @@ def tile_rbf_kernel(tc, X, X2, lengthscale, variance, out):
             nc.vector.tensor_scalar(out=arg[:], in0=arg[:], scalar1=0.0, scalar2=None, op0=ALU.min)
 
         def expo(w):
-            t, h = units[w]
+            k, h = units[w]
             arg = args[w]
-            res = rpool.tile([P, UNIT], F32, tag="res", name="res" + str(t) + "_" + str(h))
-            nc.scalar.activation(out=res[:], in_=arg[:], func=ACT.Exp, bias=lnv[:, 0:1])
-            nc.sync.dma_start(out=out_v[:, t, h * UNIT:(h + 1) * UNIT], in_=res[:])
+            res = rpool.tile([P, 2, UNIT], F32, tag="res", name="res" + str(w))
+            for part in ((slice(0, 1), slice(1, 2)) if w == nun - 1 else (slice(0, 2),)):
+                if w in by_scalar:
+                    nc.scalar.activation(out=arg[:, part, :], in_=arg[:, part, :], func=ACT.Relu, scale=-1.0)
+                    nc.scalar.activation(
+                        out=res[:, part, :], in_=arg[:, part, :], func=ACT.Exp, bias=lnv[:, 0:1], scale=-1.0
+                    )
+                else:
+                    nc.scalar.activation(out=res[:, part, :], in_=arg[:, part, :], func=ACT.Exp, bias=lnv[:, 0:1])
+                nc.sync.dma_start(
+                    out=out_v[:, 2 * k + part.start:2 * k + part.stop, h * UNIT:(h + 1) * UNIT], in_=res[:, part, :]
+                )
 
+        by_scalar = ()
         pins = tc.manual_schedule(engines={ENG.PE, ENG.DVE, ENG.Activation, ENG.Pool})
         ctx.enter_context(pins)
 
@@ -221,11 +237,13 @@ def tile_rbf_kernel(tc, X, X2, lengthscale, variance, out):
         nc.vector.scalar_tensor_tensor(out=sp[:], in0=lraw[:], scalar=0.0, in1=lp[:], op0=ALU.max, op1=ALU.add)
         rl4 = const.tile([P, 4], F32)
         nc.vector.reciprocal(out=rl4[:], in_=sp[:])
+        square(0)
         scale(0)
+        square(2)
         wpos = const.tile([P, 4], F32)
         nc.vector.scalar_tensor_tensor(out=wpos[:], in0=rl4[:], scalar=0.5, in1=rl4[:], op0=ALU.mult, op1=ALU.mult)
 
-        rlt = ps_acc.tile([P, CH], F32, tag="acc")
+        rlt = psum.tile([P, CH], F32, tag="bank")
         for ue in range(4):
             nc.tensor.transpose(
                 out=rlt[:, ue * P:(ue + 1) * P], in_=rl4[:, ue:ue + 1].to_broadcast([P, P]), identity=ident[:]
@@ -245,61 +263,59 @@ def tile_rbf_kernel(tc, X, X2, lengthscale, variance, out):
         nc.scalar.activation(out=pv[:], in_=vraw[:], func=ACT.Relu)
         lnv = const.tile([P, 1], F32)
         nc.scalar.activation(out=lnv[:], in_=lv[:], func=ACT.Ln, bias=pv[:, 0:1])
-        square(0)
 
-        for t in range(8):
-            rows_scaled(t)
+        for k in range(6):
+            rows_scaled(k)
         tpose(4)
-        norms_at = {5: (0, 1), 7: (2, 3), 9: (4, 5), 11: (6, 7)}
-        colsum_at = {4: 0, 6: 1, 8: 2, 10: 3}
+        norms_at = {5: (0, 1), 6: (2, 3), 8: (4, 5), 10: (6, 7)}
+        squares_at = {2: (4,), 4: (6,), 9: (12,), 10: (13,), 11: (14, 15)}
+        colsum_at = {2: 0, 4: 1, 6: 2, 8: 3, 11: 4}
         for i in range(1, 12):
             scale(i)
-            if order[i][0] == "y":
-                square(i)
             if i + 4 < ngr:
                 tpose(i + 4)
             if i in colsum_at:
                 colsum(colsum_at[i])
-            if i in norms_at:
-                for t in norms_at[i]:
-                    row_norm(t)
-            if i == 8:
+            for t in norms_at.get(i, ()):
+                row_norm(t)
+            if i == 6:
                 take(0)
-            if i == 11:
-                take(1)
-            if i < 5:
-                rows_scaled(7 + i)
-        for i in (0, 2, 1, 4, 6, 3, 5, 7, 8, 9, 10, 11):
-            quant(i)
+            for w in squares_at.get(i, ()):
+                square(w)
+        take(1)
+        for name, k in (("y", 0), ("x", 0), ("y", 1), ("x", 1), ("x", 2), ("x", 3)):
+            quant(name, k)
 
-        late_scale = {1: 12, 3: 13, 5: 14, 7: 15}
+        sums = [(g, ue) for g in range(5, 8) for ue in range(4)]
         mxu(0)
-        mxu(1)
         for t in range(8, 12):
             row_norm(t)
         for u in range(nun):
+            if u + 1 < nun:
+                mxu(u + 1)
             addu(u)
-            if u + 2 < nun:
-                mxu(u + 2)
-            if u in late_scale:
-                scale(late_scale[u])
-                square(late_scale[u])
-            if u in (3, 5, 7, 9):
-                colsum(4 + (u - 3) // 2)
-            if u in (7, 11):
-                take(2 + (u - 7) // 4)
-            if u < nun - 3:
-                clamp(u)
-            else:
-                clamp_v(u)
             if u < 4:
-                rows_scaled(12 + u)
-            if u >= 2:
-                expo(u - 2)
-            if 2 <= u < 6:
-                row_norm(10 + u)
-            if u == 9:
-                for i in range(12, ngr):
-                    quant(i)
-        for u in range(nun - 2, nun):
-            expo(u)
+                scale(12 + u)
+            if u < 6:
+                for g, ue in sums[2 * u:2 * u + 2]:
+                    colsum(g, (ue,))
+            if u == 3:
+                take(2)
+            if u == 6:
+                take(3)
+            if u >= nun - 2:
+                if u < nun - 1:
+                    clamp_v(u)
+            elif u not in by_scalar:
+                clamp(u)
+            if u < 2:
+                rows_scaled(6 + u)
+            if u >= 1:
+                expo(u - 1)
+            if u in (1, 2):
+                row_norm(10 + 2 * u)
+                row_norm(11 + 2 * u)
+            if u == 4:
+                quant("y", 2)
+                quant("y", 3)
+        expo(nun - 1)

@@ -172,54 +172,56 @@ def tile_rbf_kernel(tc, X, X2, lengthscale, variance, out):
                     )
                     accs[(t, c)] = acc
 
+        by_scalar = ()
+
+        def parts(w):
+            return (slice(0, 1), slice(1, 2)) if w == 0 or w >= nun - 5 else (slice(0, 2),)
+
         def addu(w):
             k, h = units[w]
             arg = apool.tile([P, 2, UNIT], F32, tag="arg", name="arg" + str(w))
             args[w] = arg
-            for a in range(2):
-                for kk in (1, 0):
-                    t, c = 2 * k + a, 2 * h + kk
-                    nc.vector.scalar_tensor_tensor(
-                        out=arg[:, a, kk * CH:(kk + 1) * CH],
-                        in0=accs[(t, c)][:],
-                        scalar=xn2[:, t:t + 1],
-                        in1=nb[:, c * CH:(c + 1) * CH],
-                        op0=ALU.subtract,
-                        op1=ALU.subtract,
+            for part in parts(w):
+                for a in range(part.start, part.stop):
+                    for kk in (1, 0):
+                        t, c = 2 * k + a, 2 * h + kk
+                        nc.vector.scalar_tensor_tensor(
+                            out=arg[:, a, kk * CH:(kk + 1) * CH],
+                            in0=accs[(t, c)][:],
+                            scalar=xn2[:, t:t + 1],
+                            in1=nb[:, c * CH:(c + 1) * CH],
+                            op0=ALU.subtract,
+                            op1=ALU.subtract,
+                        )
+                if w in by_scalar:
+                    nc.scalar.activation(out=arg[:, part, :], in_=arg[:, part, :], func=ACT.Relu, scale=-1.0)
+                elif w >= nun - 2:
+                    nc.vector.tensor_scalar(
+                        out=arg[:, part, :], in0=arg[:, part, :], scalar1=0.0, scalar2=None, op0=ALU.min
                     )
-                if w == nun - 1:
-                    nc.vector.tensor_scalar(out=arg[:, a, :], in0=arg[:, a, :], scalar1=0.0, scalar2=None, op0=ALU.min)
-
-        def clamp(w):
-            arg = args[w]
-            nc.gpsimd.tensor_scalar(out=arg[:], in0=arg[:], scalar1=0.0, scalar2=-1.0e30, op0=ALU.min, op1=ALU.max)
-
-        def clamp_v(w):
-            arg = args[w]
-            nc.vector.tensor_scalar(out=arg[:], in0=arg[:], scalar1=0.0, scalar2=None, op0=ALU.min)
+                else:
+                    nc.gpsimd.tensor_scalar(
+                        out=arg[:, part, :], in0=arg[:, part, :], scalar1=0.0, scalar2=-1.0e30, op0=ALU.min, op1=ALU.max
+                    )
 
         def expo(w):
             k, h = units[w]
             arg = args[w]
             res = rpool.tile([P, 2, UNIT], F32, tag="res", name="res" + str(w))
-            for part in ((slice(0, 1), slice(1, 2)) if w == nun - 1 else (slice(0, 2),)):
-                if w in by_scalar:
-                    nc.scalar.activation(out=arg[:, part, :], in_=arg[:, part, :], func=ACT.Relu, scale=-1.0)
-                    nc.scalar.activation(
-                        out=res[:, part, :], in_=arg[:, part, :], func=ACT.Exp, bias=lnv[:, 0:1], scale=-1.0
-                    )
-                else:
-                    nc.scalar.activation(out=res[:, part, :], in_=arg[:, part, :], func=ACT.Exp, bias=lnv[:, 0:1])
+            for part in parts(w):
+                nc.scalar.activation(
+                    out=res[:, part, :], in_=arg[:, part, :], func=ACT.Exp, bias=lnv[:, 0:1],
+                    scale=-1.0 if w in by_scalar else 1.0,
+                )
                 nc.sync.dma_start(
                     out=out_v[:, 2 * k + part.start:2 * k + part.stop, h * UNIT:(h + 1) * UNIT], in_=res[:, part, :]
                 )
 
-        by_scalar = ()
         pins = tc.manual_schedule(engines={ENG.PE, ENG.DVE, ENG.Activation, ENG.Pool})
         ctx.enter_context(pins)
 
-        for i in range(4):
-            tpose(i)
+        tpose(0)
+        tpose(1)
 
         one = const.tile([P, 4], F32)
         nc.vector.memset(one[:], 1.0)
@@ -231,6 +233,10 @@ def tile_rbf_kernel(tc, X, X2, lengthscale, variance, out):
         nc.vector.scalar_tensor_tensor(out=nl[:], in0=lraw[:], scalar=-1.0, in1=lraw[:], op0=ALU.mult, op1=ALU.min)
         ex = const.tile([P, 4], F32)
         nc.gpsimd.tensor_tensor(out=ex[:], in0=base[:], in1=nl[:], op=ALU.pow)
+        nv = const.tile([P, 1], F32)
+        nc.vector.scalar_tensor_tensor(out=nv[:], in0=vraw[:], scalar=-1.0, in1=vraw[:], op0=ALU.mult, op1=ALU.min)
+        ev = const.tile([P, 1], F32)
+        nc.gpsimd.tensor_tensor(out=ev[:], in0=base[:, 0:1], in1=nv[:], op=ALU.pow)
         lp = const.tile([P, 4], F32)
         nc.scalar.activation(out=lp[:], in_=ex[:], func=ACT.Ln, bias=1.0)
         sp = const.tile([P, 4], F32)
@@ -238,8 +244,8 @@ def tile_rbf_kernel(tc, X, X2, lengthscale, variance, out):
         rl4 = const.tile([P, 4], F32)
         nc.vector.reciprocal(out=rl4[:], in_=sp[:])
         square(0)
+        scale(1)
         scale(0)
-        square(2)
         wpos = const.tile([P, 4], F32)
         nc.vector.scalar_tensor_tensor(out=wpos[:], in0=rl4[:], scalar=0.5, in1=rl4[:], op0=ALU.mult, op1=ALU.mult)
 
@@ -248,41 +254,42 @@ def tile_rbf_kernel(tc, X, X2, lengthscale, variance, out):
             nc.tensor.transpose(
                 out=rlt[:, ue * P:(ue + 1) * P], in_=rl4[:, ue:ue + 1].to_broadcast([P, P]), identity=ident[:]
             )
+        tpose(2)
+        tpose(3)
         rlb = const.tile([P, D], F32)
         nc.scalar.copy(
             out=rlb[:].rearrange("m (u q e) -> m u q e", u=2, e=2),
             in_=rlt[:].rearrange("m (u e q) -> m u q e", u=2, e=2),
         )
-        nv = const.tile([P, 1], F32)
-        nc.vector.scalar_tensor_tensor(out=nv[:], in0=vraw[:], scalar=-1.0, in1=vraw[:], op0=ALU.mult, op1=ALU.min)
-        ev = const.tile([P, 1], F32)
-        nc.gpsimd.tensor_tensor(out=ev[:], in0=base[:, 0:1], in1=nv[:], op=ALU.pow)
         lv = const.tile([P, 1], F32)
         nc.scalar.activation(out=lv[:], in_=ev[:], func=ACT.Ln, bias=1.0)
         pv = const.tile([P, 1], F32)
         nc.scalar.activation(out=pv[:], in_=vraw[:], func=ACT.Relu)
         lnv = const.tile([P, 1], F32)
         nc.scalar.activation(out=lnv[:], in_=lv[:], func=ACT.Ln, bias=pv[:, 0:1])
+        nc.scalar.activation(out=warm[:], in_=one[:], func=ACT.Exp)
 
-        for k in range(6):
+        for k in range(8):
             rows_scaled(k)
         tpose(4)
         norms_at = {5: (0, 1), 6: (2, 3), 8: (4, 5), 10: (6, 7)}
-        squares_at = {2: (4,), 4: (6,), 9: (12,), 10: (13,), 11: (14, 15)}
-        colsum_at = {2: 0, 4: 1, 6: 2, 8: 3, 11: 4}
+        squares_at = {2: (2,), 4: (4,), 6: (6,), 9: (12,), 10: (13,), 11: (14, 15)}
+        colsum_at = {2: 0, 5: 1, 7: 2, 9: 3, 11: 4}
         for i in range(1, 12):
-            scale(i)
+            if i > 1:
+                scale(i)
             if i + 4 < ngr:
                 tpose(i + 4)
             if i in colsum_at:
                 colsum(colsum_at[i])
             for t in norms_at.get(i, ()):
                 row_norm(t)
-            if i == 6:
+            if i == 7:
                 take(0)
+            if i == 11:
+                take(1)
             for w in squares_at.get(i, ()):
                 square(w)
-        take(1)
         for name, k in (("y", 0), ("x", 0), ("y", 1), ("x", 1), ("x", 2), ("x", 3)):
             quant(name, k)
 
@@ -303,13 +310,6 @@ def tile_rbf_kernel(tc, X, X2, lengthscale, variance, out):
                 take(2)
             if u == 6:
                 take(3)
-            if u >= nun - 2:
-                if u < nun - 1:
-                    clamp_v(u)
-            elif u not in by_scalar:
-                clamp(u)
-            if u < 2:
-                rows_scaled(6 + u)
             if u >= 1:
                 expo(u - 1)
             if u in (1, 2):

@@ -29,7 +29,7 @@ def tile_rbf_kernel(tc, X, X2, lengthscale, variance, out):
         const = ctx.enter_context(tc.tile_pool(name="const", bufs=1))
         stage = ctx.enter_context(tc.tile_pool(name="stage", bufs=8))
         upool = ctx.enter_context(tc.tile_pool(name="upool", bufs=5))
-        gpool = ctx.enter_context(tc.tile_pool(name="gpool", bufs=8))
+        gpool = ctx.enter_context(tc.tile_pool(name="gpool", bufs=4))
         apool = ctx.enter_context(tc.tile_pool(name="apool", bufs=5))
         rpool = ctx.enter_context(tc.tile_pool(name="rpool", bufs=4))
         psum = ctx.enter_context(tc.psum_pool(name="psum", bufs=8))
@@ -63,6 +63,7 @@ def tile_rbf_kernel(tc, X, X2, lengthscale, variance, out):
             codes[name] = const.tile([P, ROWS], U32, name="codes_" + name, align_bytes=64)
             scls[name] = const.tile([P, ROWS], U8, name="scls_" + name, align_bytes=64)
         xn2 = const.tile([P, TILES], F32)
+        xr = const.tile([P, CH], F32)
         junk = const.tile([P, D], BF16)
         nb = const.tile([P, ROWS], F32)
         grps = {}
@@ -92,12 +93,12 @@ def tile_rbf_kernel(tc, X, X2, lengthscale, variance, out):
 
         def scale(i):
             name, g = order[i]
-            if (name, g // 2) not in grps:
-                grp = gpool.tile([P, 8 * GCOLS], BF16, tag="grp", name="grp_" + name + str(g), align_bytes=64)
-                grps[(name, g // 2)] = grp
-            grp = grps[(name, g // 2)]
+            if (name, g // 4) not in grps:
+                grp = gpool.tile([P, 16 * GCOLS], BF16, tag="grp", name="grp_" + name + str(g), align_bytes=64)
+                grps[(name, g // 4)] = grp
+            grp = grps[(name, g // 4)]
             nc.vector.tensor_tensor(
-                out=grp[:, (g % 2) * 4 * GCOLS:(g % 2 + 1) * 4 * GCOLS].rearrange("q (r u e) -> q r u e", u=2, e=2),
+                out=grp[:, (g % 4) * 4 * GCOLS:(g % 4 + 1) * 4 * GCOLS].rearrange("q (r u e) -> q r u e", u=2, e=2),
                 in0=trs[i][:].bitcast(BF16).rearrange("q (u r e) -> q r u e", u=2, e=2),
                 in1=rl4[:].rearrange("q (u e) -> q u e", e=2).unsqueeze(1).to_broadcast([P, GCOLS, 2, 2]),
                 op=ALU.mult,
@@ -111,24 +112,38 @@ def tile_rbf_kernel(tc, X, X2, lengthscale, variance, out):
                 in_=trs[i][:].bitcast(BF16).rearrange("q (u r e) -> q u e r", u=2, e=2),
                 func=ACT.Square,
             )
-            sqs[g] = sq
+            sqs[(name, g)] = sq
 
-        def colsum(g, ues=range(4)):
+        def colsum(name, g, ues=range(4)):
             if g % 2 == 0 and 0 in ues:
-                acc = psum.tile([P, CH], F32, tag="bank", name="nps" + str(g))
-                nps[g // 2] = acc
-            acc = nps[g // 2]
+                acc = psum.tile([P, CH], F32, tag="bank", name="nps_" + name + str(g))
+                nps[(name, g // 2)] = acc
+            acc = nps[(name, g // 2)]
             for ue in ues:
                 nc.tensor.matmul(
                     out=acc[:, (g % 2) * GCOLS:(g % 2 + 1) * GCOLS],
                     lhsT=wpos[:, ue:ue + 1].to_broadcast([P, P]),
-                    rhs=sqs[g][:, ue, :],
+                    rhs=sqs[(name, g)][:, ue, :],
                     start=(ue == 0),
                     stop=(ue == 3),
                 )
 
         def take(k):
-            nc.scalar.copy(out=nb[:, k * CH:(k + 1) * CH], in_=nps[k][:])
+            nc.scalar.copy(out=nb[:, k * CH:(k + 1) * CH], in_=nps[("y", k)][:])
+
+        def xrow():
+            nc.scalar.copy(out=xr[:], in_=nps[("x", 3)][:])
+
+        def xturn():
+            turned = psum.tile([P, CH], F32, tag="bank", name="turned")
+            for j in range(4):
+                nc.tensor.transpose(
+                    out=turned[:, j * P:(j + 1) * P], in_=xr[:, j * P:(j + 1) * P], identity=ident[:]
+                )
+            nps["turned"] = turned
+
+        def xtake():
+            nc.scalar.copy(out=xn2[:, 12:16], in_=nps["turned"][:].rearrange("p (j c) -> p j c", c=P)[:, :, 0])
 
         def rows_scaled(k):
             u32 = upool.tile([P, 2, D], F32, tag="u32", name="u32_" + str(k))
@@ -143,7 +158,7 @@ def tile_rbf_kernel(tc, X, X2, lengthscale, variance, out):
             )
 
         def quant(name, k):
-            cols = slice(k * 2 * GCOLS, (k + 1) * 2 * GCOLS)
+            cols = slice(k * 4 * GCOLS, (k + 1) * 4 * GCOLS)
             nc.vector.quantize_mx(
                 out=codes[name][:, cols].bitcast(FP8X4),
                 scales=scls[name][:, cols],
@@ -195,7 +210,7 @@ def tile_rbf_kernel(tc, X, X2, lengthscale, variance, out):
                         )
                 if w in by_scalar:
                     nc.scalar.activation(out=arg[:, part, :], in_=arg[:, part, :], func=ACT.Relu, scale=-1.0)
-                elif w >= nun - 2:
+                elif w == nun - 1:
                     nc.vector.tensor_scalar(
                         out=arg[:, part, :], in0=arg[:, part, :], scalar1=0.0, scalar2=None, op0=ALU.min
                     )
@@ -269,19 +284,19 @@ def tile_rbf_kernel(tc, X, X2, lengthscale, variance, out):
         nc.scalar.activation(out=lnv[:], in_=lv[:], func=ACT.Ln, bias=pv[:, 0:1])
         nc.scalar.activation(out=warm[:], in_=one[:], func=ACT.Exp)
 
-        for k in range(8):
+        for k in range(5):
             rows_scaled(k)
         tpose(4)
-        norms_at = {5: (0, 1), 6: (2, 3), 8: (4, 5), 10: (6, 7)}
-        squares_at = {2: (2,), 4: (4,), 6: (6,), 9: (12,), 10: (13,), 11: (14, 15)}
-        colsum_at = {2: 0, 5: 1, 7: 2, 9: 3, 11: 4}
+        norms_at = {5: (0, 1), 6: (2, 3), 8: (4, 5), 9: (6, 7)}
+        squares_at = {2: (2,), 4: (4,), 6: (6,), 10: (10,), 11: (11, 12)}
+        colsum_at = {2: 0, 5: 1, 7: 2, 9: 3}
         for i in range(1, 12):
             if i > 1:
                 scale(i)
             if i + 4 < ngr:
                 tpose(i + 4)
             if i in colsum_at:
-                colsum(colsum_at[i])
+                colsum("y", colsum_at[i])
             for t in norms_at.get(i, ()):
                 row_norm(t)
             if i == 7:
@@ -290,13 +305,16 @@ def tile_rbf_kernel(tc, X, X2, lengthscale, variance, out):
                 take(1)
             for w in squares_at.get(i, ()):
                 square(w)
-        for name, k in (("y", 0), ("x", 0), ("y", 1), ("x", 1), ("x", 2), ("x", 3)):
+        for name, k in (("y", 0), ("x", 0), ("x", 1)):
             quant(name, k)
 
-        sums = [(g, ue) for g in range(5, 8) for ue in range(4)]
+        sums = [("x", 7, ue) for ue in range(4)] + [("y", g, ue) for g in range(4, 8) for ue in range(4)]
+        ends = (3, 7, 11, 14, 18, 20)
         mxu(0)
-        for t in range(8, 12):
-            row_norm(t)
+        colsum("x", 6)
+        row_norm(8)
+        row_norm(9)
+        square(13)
         for u in range(nun):
             if u + 1 < nun:
                 mxu(u + 1)
@@ -304,18 +322,28 @@ def tile_rbf_kernel(tc, X, X2, lengthscale, variance, out):
             if u < 4:
                 scale(12 + u)
             if u < 6:
-                for g, ue in sums[2 * u:2 * u + 2]:
-                    colsum(g, (ue,))
+                for name, g, ue in sums[ends[u - 1] if u else 0:ends[u]]:
+                    colsum(name, g, (ue,))
+            if u == 0:
+                rows_scaled(5)
+                square(14)
+            if u == 1:
+                expo(0)
+                row_norm(10)
+                row_norm(11)
+                square(15)
+            if u == 2:
+                xrow()
             if u == 3:
+                xturn()
+            if u == 4:
                 take(2)
+            if u == 5:
+                xtake()
             if u == 6:
                 take(3)
-            if u >= 1:
+            if u >= 2:
                 expo(u - 1)
-            if u in (1, 2):
-                row_norm(10 + 2 * u)
-                row_norm(11 + 2 * u)
             if u == 4:
-                quant("y", 2)
-                quant("y", 3)
+                quant("y", 1)
         expo(nun - 1)

@@ -36,7 +36,7 @@ def tile_rbf_kernel(tc, X, X2, lengthscale, variance, out):
 
         lraw = const.tile([P, 4], BF16)
         vraw = const.tile([P, 1], BF16)
-        nc.sync.dma_start(
+        nc.scalar.dma_start(
             out=lraw[:].rearrange("q (u e) -> q u e", e=2),
             in_=lengthscale.rearrange("o (u q e) -> (o q) u e", u=2, e=2),
         )
@@ -187,10 +187,8 @@ def tile_rbf_kernel(tc, X, X2, lengthscale, variance, out):
                     )
                     accs[(t, c)] = acc
 
-        by_scalar = ()
-
         def parts(w):
-            return (slice(0, 1), slice(1, 2)) if w == 0 or w >= nun - 5 else (slice(0, 2),)
+            return (slice(0, 1), slice(1, 2)) if w == 0 or w >= nun - 3 else (slice(0, 2),)
 
         def addu(w):
             k, h = units[w]
@@ -208,9 +206,7 @@ def tile_rbf_kernel(tc, X, X2, lengthscale, variance, out):
                             op0=ALU.subtract,
                             op1=ALU.subtract,
                         )
-                if w in by_scalar:
-                    nc.scalar.activation(out=arg[:, part, :], in_=arg[:, part, :], func=ACT.Relu, scale=-1.0)
-                elif w == nun - 1:
+                if w == nun - 1:
                     nc.vector.tensor_scalar(
                         out=arg[:, part, :], in0=arg[:, part, :], scalar1=0.0, scalar2=None, op0=ALU.min
                     )
@@ -224,13 +220,15 @@ def tile_rbf_kernel(tc, X, X2, lengthscale, variance, out):
             arg = args[w]
             res = rpool.tile([P, 2, UNIT], F32, tag="res", name="res" + str(w))
             for part in parts(w):
-                nc.scalar.activation(
-                    out=res[:, part, :], in_=arg[:, part, :], func=ACT.Exp, bias=lnv[:, 0:1],
-                    scale=-1.0 if w in by_scalar else 1.0,
-                )
-                nc.sync.dma_start(
-                    out=out_v[:, 2 * k + part.start:2 * k + part.stop, h * UNIT:(h + 1) * UNIT], in_=res[:, part, :]
-                )
+                last = w == nun - 1 and part.stop == 2
+                for lo, hi in ((0, CH), (CH, UNIT)) if last else ((0, UNIT),):
+                    nc.scalar.activation(
+                        out=res[:, part, lo:hi], in_=arg[:, part, lo:hi], func=ACT.Exp, bias=lnv[:, 0:1]
+                    )
+                    nc.sync.dma_start(
+                        out=out_v[:, 2 * k + part.start:2 * k + part.stop, h * UNIT + lo:h * UNIT + hi],
+                        in_=res[:, part, lo:hi],
+                    )
 
         pins = tc.manual_schedule(engines={ENG.PE, ENG.DVE, ENG.Activation, ENG.Pool})
         ctx.enter_context(pins)

@@ -36,7 +36,7 @@ def tile_rbf_kernel(tc, X, X2, lengthscale, variance, out):
 
         lraw = const.tile([P, 4], BF16)
         vraw = const.tile([P, 1], BF16)
-        nc.scalar.dma_start(
+        nc.sync.dma_start(
             out=lraw[:].rearrange("q (u e) -> q u e", e=2),
             in_=lengthscale.rearrange("o (u q e) -> (o q) u e", u=2, e=2),
         )
@@ -63,7 +63,7 @@ def tile_rbf_kernel(tc, X, X2, lengthscale, variance, out):
             codes[name] = const.tile([P, ROWS], U32, name="codes_" + name, align_bytes=64)
             scls[name] = const.tile([P, ROWS], U8, name="scls_" + name, align_bytes=64)
         xn2 = const.tile([P, TILES], F32)
-        xr = const.tile([P, CH], F32)
+        xr = const.tile([P, GCOLS], F32)
         junk = const.tile([P, D], BF16)
         nb = const.tile([P, ROWS], F32)
         grps = {}
@@ -115,7 +115,7 @@ def tile_rbf_kernel(tc, X, X2, lengthscale, variance, out):
             sqs[(name, g)] = sq
 
         def colsum(name, g, ues=range(4)):
-            if g % 2 == 0 and 0 in ues:
+            if (name, g // 2) not in nps:
                 acc = psum.tile([P, CH], F32, tag="bank", name="nps_" + name + str(g))
                 nps[(name, g // 2)] = acc
             acc = nps[(name, g // 2)]
@@ -132,18 +132,20 @@ def tile_rbf_kernel(tc, X, X2, lengthscale, variance, out):
             nc.scalar.copy(out=nb[:, k * CH:(k + 1) * CH], in_=nps[("y", k)][:])
 
         def xrow():
-            nc.scalar.copy(out=xr[:], in_=nps[("x", 3)][:])
+            nc.scalar.copy(out=xr[:], in_=nps[("x", 3)][:, GCOLS:CH])
 
         def xturn():
             turned = psum.tile([P, CH], F32, tag="bank", name="turned")
-            for j in range(4):
+            for j in range(2):
                 nc.tensor.transpose(
                     out=turned[:, j * P:(j + 1) * P], in_=xr[:, j * P:(j + 1) * P], identity=ident[:]
                 )
             nps["turned"] = turned
 
         def xtake():
-            nc.scalar.copy(out=xn2[:, 12:16], in_=nps["turned"][:].rearrange("p (j c) -> p j c", c=P)[:, :, 0])
+            nc.scalar.copy(
+                out=xn2[:, TILES - 2:TILES], in_=nps["turned"][:, 0:GCOLS].rearrange("p (j c) -> p j c", c=P)[:, :, 0]
+            )
 
         def rows_scaled(k):
             u32 = upool.tile([P, 2, D], F32, tag="u32", name="u32_" + str(k))
@@ -286,7 +288,7 @@ def tile_rbf_kernel(tc, X, X2, lengthscale, variance, out):
             rows_scaled(k)
         tpose(4)
         norms_at = {5: (0, 1), 6: (2, 3), 8: (4, 5), 9: (6, 7)}
-        squares_at = {2: (2,), 4: (4,), 6: (6,), 10: (10,), 11: (11, 12)}
+        squares_at = {2: (2,), 4: (4,), 6: (6,), 11: (11, 12)}
         colsum_at = {2: 0, 5: 1, 7: 2, 9: 3}
         for i in range(1, 12):
             if i > 1:
@@ -307,12 +309,12 @@ def tile_rbf_kernel(tc, X, X2, lengthscale, variance, out):
             quant(name, k)
 
         sums = [("x", 7, ue) for ue in range(4)] + [("y", g, ue) for g in range(4, 8) for ue in range(4)]
-        ends = (3, 7, 11, 14, 18, 20)
+        ends = (4, 7, 11, 15, 19, 20)
         mxu(0)
-        colsum("x", 6)
         row_norm(8)
         row_norm(9)
         square(13)
+        square(14)
         for u in range(nun):
             if u + 1 < nun:
                 mxu(u + 1)
@@ -322,14 +324,8 @@ def tile_rbf_kernel(tc, X, X2, lengthscale, variance, out):
             if u < 6:
                 for name, g, ue in sums[ends[u - 1] if u else 0:ends[u]]:
                     colsum(name, g, (ue,))
-            if u == 0:
-                rows_scaled(5)
-                square(14)
-            if u == 1:
-                expo(0)
-                row_norm(10)
-                row_norm(11)
-                square(15)
+            if u < 2:
+                rows_scaled(5 + u)
             if u == 2:
                 xrow()
             if u == 3:
@@ -340,8 +336,15 @@ def tile_rbf_kernel(tc, X, X2, lengthscale, variance, out):
                 xtake()
             if u == 6:
                 take(3)
-            if u >= 2:
+            if u >= 1:
                 expo(u - 1)
+            if u == 1:
+                row_norm(10)
+                row_norm(11)
+                square(15)
+            if u == 2:
+                row_norm(12)
+                row_norm(13)
             if u == 4:
                 quant("y", 1)
         expo(nun - 1)

@@ -208,29 +208,23 @@ def tile_rbf_kernel(tc, X, X2, lengthscale, variance, out):
                             op0=ALU.subtract,
                             op1=ALU.subtract,
                         )
-                if w == nun - 1:
-                    nc.vector.tensor_scalar(
-                        out=arg[:, part, :], in0=arg[:, part, :], scalar1=0.0, scalar2=None, op0=ALU.min
-                    )
-                else:
+                if w < nun - 1:
                     nc.gpsimd.tensor_scalar(
                         out=arg[:, part, :], in0=arg[:, part, :], scalar1=0.0, scalar2=-1.0e30, op0=ALU.min, op1=ALU.max
                     )
+
+            if w == nun - 1:
+                nc.vector.tensor_scalar(out=arg[:], in0=arg[:], scalar1=0.0, scalar2=None, op0=ALU.min)
 
         def expo(w):
             k, h = units[w]
             arg = args[w]
             res = rpool.tile([P, 2, UNIT], F32, tag="res", name="res" + str(w))
             for part in parts(w):
-                last = w == nun - 1 and part.stop == 2
-                for lo, hi in ((0, CH), (CH, UNIT)) if last else ((0, UNIT),):
-                    nc.scalar.activation(
-                        out=res[:, part, lo:hi], in_=arg[:, part, lo:hi], func=ACT.Exp, bias=lnv[:, 0:1]
-                    )
-                    nc.sync.dma_start(
-                        out=out_v[:, 2 * k + part.start:2 * k + part.stop, h * UNIT + lo:h * UNIT + hi],
-                        in_=res[:, part, lo:hi],
-                    )
+                nc.scalar.activation(out=res[:, part, :], in_=arg[:, part, :], func=ACT.Exp, bias=lnv[:, 0:1])
+                nc.sync.dma_start(
+                    out=out_v[:, 2 * k + part.start:2 * k + part.stop, h * UNIT:(h + 1) * UNIT], in_=res[:, part, :]
+                )
 
         pins = tc.manual_schedule(engines={ENG.PE, ENG.DVE, ENG.Activation, ENG.Pool})
         ctx.enter_context(pins)

import math
from contextlib import ExitStack

import concourse.mybir as mybir
from concourse.masks import make_identity

F32 = mybir.dt.float32
BF16 = mybir.dt.bfloat16
U32 = mybir.dt.uint32
U8 = mybir.dt.uint8
FP8X4 = mybir.dt.float8_e4m3fn_x4
ALU = mybir.AluOpType
ACT = mybir.ActivationFunctionType
ENG = mybir.EngineType

P = 128
ROWS = 2048
D = 512
TILES = ROWS // P
GCOLS = 2 * P
CH = 512
UNIT = 2 * CH
FLOPS = 2 * ROWS * ROWS * D


def tile_rbf_kernel(tc, X, X2, lengthscale, variance, out):
    nc = tc.nc
    with ExitStack() as ctx:
        const = ctx.enter_context(tc.tile_pool(name="const", bufs=1))
        stage = ctx.enter_context(tc.tile_pool(name="stage", bufs=8))
        upool = ctx.enter_context(tc.tile_pool(name="upool", bufs=5))
        gpool = ctx.enter_context(tc.tile_pool(name="gpool", bufs=4))
        apool = ctx.enter_context(tc.tile_pool(name="apool", bufs=5))
        rpool = ctx.enter_context(tc.tile_pool(name="rpool", bufs=4))
        psum = ctx.enter_context(tc.psum_pool(name="psum", bufs=8))

        lraw = const.tile([P, 4], BF16)
        vraw = const.tile([P, 1], BF16)
        nc.sync.dma_start(
            out=lraw[:].rearrange("q (u e) -> q u e", e=2),
            in_=lengthscale.rearrange("o (u q e) -> (o q) u e", u=2, e=2),
        )
        x2_raw = const.tile([P, TILES, D], BF16)
        x_raw = const.tile([P, TILES, D], BF16)
        x2_v = X2.rearrange("(c p) f -> p c f", p=P)
        x_v = X.rearrange("(t p) f -> p t f", p=P)
        out_v = out.rearrange("(t p) j -> p t j", p=P)
        for raw, view, lo, hi in (
            (x2_raw, x2_v, 0, 2), (x_raw, x_v, 0, 2), (x2_raw, x2_v, 2, 4), (x_raw, x_v, 2, 4),
            (x2_raw, x2_v, 4, 8), (x_raw, x_v, 4, 8),
            (x_raw, x_v, 8, 12), (x_raw, x_v, 12, 16), (x2_raw, x2_v, 8, 12), (x2_raw, x2_v, 12, 16),
        ):
            nc.sync.dma_start(out=raw[:, lo:hi, :], in_=view[:, lo:hi, :])
        nc.scalar.dma_start(out=vraw[:], in_=variance.partition_broadcast(P))
        raws = {"x": x_raw, "y": x2_raw}

        ident = const.tile([P, P], F32)
        make_identity(nc, ident[:])

        codes = {}
        scls = {}
        for name in ("x", "y"):
            codes[name] = const.tile([P, ROWS], U32, name="codes_" + name, align_bytes=64)
            scls[name] = const.tile([P, ROWS], U8, name="scls_" + name, align_bytes=64)
        xn2 = const.tile([P, TILES], F32)
        xr = const.tile([P, GCOLS], F32)
        junk = const.tile([P, D], BF16)
        nb = const.tile([P, ROWS], F32)
        grps = {}
        trs = {}
        sqs = {}
        nps = {}
        u32s = {}

        order = (
            ("y", 0), ("x", 0), ("y", 1), ("x", 1), ("y", 2), ("x", 2), ("y", 3), ("x", 3),
            ("x", 4), ("x", 5), ("x", 6), ("x", 7), ("y", 4), ("y", 5), ("y", 6), ("y", 7),
        )
        ngr = len(order)

        def tpose(i):
            name, g = order[i]
            words = raws[name][:].bitcast(F32)
            tr = psum.tile([P, CH], F32, tag="bank", name="tr_" + name + str(g))
            for a in range(2):
                for u in range(2):
                    nc.tensor.transpose(
                        out=tr[:, u * GCOLS + a * P:u * GCOLS + (a + 1) * P],
                        in_=words[:, 2 * g + a, u * P:(u + 1) * P],
                        identity=ident[:],
                    )
            trs[i] = tr

        def scale(i):
            name, g = order[i]
            if (name, g // 4) not in grps:
                grp = gpool.tile([P, 16 * GCOLS], BF16, tag="grp", name="grp_" + name + str(g), align_bytes=64)
                grps[(name, g // 4)] = grp
            grp = grps[(name, g // 4)]
            nc.vector.tensor_tensor(
                out=grp[:, (g % 4) * 4 * GCOLS:(g % 4 + 1) * 4 * GCOLS].rearrange("q (r u e) -> q r u e", u=2, e=2),
                in0=trs[i][:].bitcast(BF16).rearrange("q (u r e) -> q r u e", u=2, e=2),
                in1=rl4[:].rearrange("q (u e) -> q u e", e=2).unsqueeze(1).to_broadcast([P, GCOLS, 2, 2]),
                op=ALU.mult,
            )

        def square(i):
            name, g = order[i]
            sq = stage.tile([P, 4, GCOLS], F32, tag="sq", name="sq_" + name + str(g))
            nc.scalar.activation(
                out=sq[:].rearrange("q (u e) r -> q u e r", e=2),
                in_=trs[i][:].bitcast(BF16).rearrange("q (u r e) -> q u e r", u=2, e=2),
                func=ACT.Square,
            )
            sqs[(name, g)] = sq

        def colsum(name, g, ues=range(4)):
            if (name, g // 2) not in nps:
                acc = psum.tile([P, CH], F32, tag="bank", name="nps_" + name + str(g))
                nps[(name, g // 2)] = acc
            acc = nps[(name, g // 2)]
            for ue in ues:
                nc.tensor.matmul(
                    out=acc[:, (g % 2) * GCOLS:(g % 2 + 1) * GCOLS],
                    lhsT=wpos[:, ue:ue + 1].to_broadcast([P, P]),
                    rhs=sqs[(name, g)][:, ue, :],
                    start=(ue == 0),
                    stop=(ue == 3),
                )

        def take(k):
            nc.scalar.copy(out=nb[:, k * CH:(k + 1) * CH], in_=nps[("y", k)][:])

        def xrow():
            nc.scalar.copy(out=xr[:], in_=nps[("x", 3)][:, GCOLS:CH])

        def xturn():
            turned = psum.tile([P, CH], F32, tag="bank", name="turned")
            for j in range(2):
                nc.tensor.transpose(
                    out=turned[:, j * P:(j + 1) * P], in_=xr[:, j * P:(j + 1) * P], identity=ident[:]
                )
            nps["turned"] = turned

        def xtake():
            nc.scalar.copy(
                out=xn2[:, TILES - 2:TILES], in_=nps["turned"][:, 0:GCOLS].rearrange("p (j c) -> p j c", c=P)[:, :, 0]
            )

        def rows_scaled(k):
            u32 = upool.tile([P, 2, D], F32, tag="u32", name="u32_" + str(k))
            nc.gpsimd.tensor_tensor(
                out=u32[:], in0=x_raw[:, 2 * k:2 * k + 2, :], in1=rlb[:].unsqueeze(1).to_broadcast([P, 2, D]), op=ALU.mult
            )
            u32s[k] = u32

        def row_norm(t):
            nc.scalar.activation(
                out=junk[:], in_=u32s[t // 2][:, t % 2, :], func=ACT.Square, scale=math.sqrt(0.5), accum_out=xn2[:, t:t + 1]
            )

        def quant(name, k):
            cols = slice(k * 4 * GCOLS, (k + 1) * 4 * GCOLS)
            nc.vector.quantize_mx(
                out=codes[name][:, cols].bitcast(FP8X4),
                scales=scls[name][:, cols],
                in_=grps[(name, k)][:],
            )

        accs = {}
        args = {}
        units = [(k, h) for h in range(2) for k in range(TILES // 2)]
        nun = len(units)

        def mxu(w):
            k, h = units[w]
            for a in range(2):
                for kk in range(2):
                    t, c = 2 * k + a, 2 * h + kk
                    acc = psum.tile([P, CH], F32, tag="bank", name="acc" + str(t) + "_" + str(c))
                    nc.tensor.matmul_mx(
                        out=acc[:],
                        lhsT=codes["x"][:, t * P:(t + 1) * P].bitcast(FP8X4),
                        lhsT_scale=scls["x"][:, t * P:(t + 1) * P],
                        rhs=codes["y"][:, c * CH:(c + 1) * CH].bitcast(FP8X4),
                        rhs_scale=scls["y"][:, c * CH:(c + 1) * CH],
                        start=True,
                        stop=True,
                    )
                    accs[(t, c)] = acc

        def parts(w):
            return (slice(0, 1), slice(1, 2)) if w == 0 or w >= nun - 3 else (slice(0, 2),)

        def addu(w):
            k, h = units[w]
            arg = apool.tile([P, 2, UNIT], F32, tag="arg", name="arg" + str(w))
            args[w] = arg
            for part in parts(w):
                for a in range(part.start, part.stop):
                    for kk in (1, 0):
                        t, c = 2 * k + a, 2 * h + kk
                        nc.vector.scalar_tensor_tensor(
                            out=arg[:, a, kk * CH:(kk + 1) * CH],
                            in0=accs[(t, c)][:],
                            scalar=xn2[:, t:t + 1],
                            in1=nb[:, c * CH:(c + 1) * CH],
                            op0=ALU.subtract,
                            op1=ALU.subtract,
                        )
                if w < nun - 1:
                    nc.gpsimd.tensor_scalar(
                        out=arg[:, part, :], in0=arg[:, part, :], scalar1=0.0, scalar2=-1.0e30, op0=ALU.min, op1=ALU.max
                    )

            if w == nun - 1:
                nc.vector.tensor_scalar(out=arg[:], in0=arg[:], scalar1=0.0, scalar2=None, op0=ALU.min)

        def expo(w):
            k, h = units[w]
            arg = args[w]
            res = rpool.tile([P, 2, UNIT], F32, tag="res", name="res" + str(w))
            for part in parts(w):
                nc.scalar.activation(out=res[:, part, :], in_=arg[:, part, :], func=ACT.Exp, bias=lnv[:, 0:1])
                nc.sync.dma_start(
                    out=out_v[:, 2 * k + part.start:2 * k + part.stop, h * UNIT:(h + 1) * UNIT], in_=res[:, part, :]
                )

        pins = tc.manual_schedule(engines={ENG.PE, ENG.DVE, ENG.Activation, ENG.Pool})
        ctx.enter_context(pins)

        tpose(0)
        tpose(1)

        one = const.tile([P, 4], F32)
        nc.vector.memset(one[:], 1.0)
        warm = const.tile([P, 4], F32)
        nc.scalar.activation(out=warm[:], in_=one[:], func=ACT.Ln)
        base = const.tile([P, 4], F32)
        nc.gpsimd.tensor_scalar(out=base[:], in0=one[:], scalar1=math.e, scalar2=None, op0=ALU.mult)
        nl = const.tile([P, 4], F32)
        nc.vector.scalar_tensor_tensor(out=nl[:], in0=lraw[:], scalar=-1.0, in1=lraw[:], op0=ALU.mult, op1=ALU.min)
        ex = const.tile([P, 4], F32)
        nc.gpsimd.tensor_tensor(out=ex[:], in0=base[:], in1=nl[:], op=ALU.pow)
        nv = const.tile([P, 1], F32)
        nc.vector.scalar_tensor_tensor(out=nv[:], in0=vraw[:], scalar=-1.0, in1=vraw[:], op0=ALU.mult, op1=ALU.min)
        ev = const.tile([P, 1], F32)
        nc.gpsimd.tensor_tensor(out=ev[:], in0=base[:, 0:1], in1=nv[:], op=ALU.pow)
        lp = const.tile([P, 4], F32)
        nc.scalar.activation(out=lp[:], in_=ex[:], func=ACT.Ln, bias=1.0)
        sp = const.tile([P, 4], F32)
        nc.vector.scalar_tensor_tensor(out=sp[:], in0=lraw[:], scalar=0.0, in1=lp[:], op0=ALU.max, op1=ALU.add)
        rl4 = const.tile([P, 4], F32)
        nc.vector.reciprocal(out=rl4[:], in_=sp[:])
        square(0)
        scale(1)
        scale(0)
        wpos = const.tile([P, 4], F32)
        nc.vector.scalar_tensor_tensor(out=wpos[:], in0=rl4[:], scalar=0.5, in1=rl4[:], op0=ALU.mult, op1=ALU.mult)

        rlt = psum.tile([P, CH], F32, tag="bank")
        for ue in range(4):
            nc.tensor.transpose(
                out=rlt[:, ue * P:(ue + 1) * P], in_=rl4[:, ue:ue + 1].to_broadcast([P, P]), identity=ident[:]
            )
        tpose(2)
        tpose(3)
        rlb = const.tile([P, D], F32)
        nc.scalar.copy(
            out=rlb[:].rearrange("m (u q e) -> m u q e", u=2, e=2),
            in_=rlt[:].rearrange("m (u e q) -> m u q e", u=2, e=2),
        )
        lv = const.tile([P, 1], F32)
        nc.scalar.activation(out=lv[:], in_=ev[:], func=ACT.Ln, bias=1.0)
        pv = const.tile([P, 1], F32)
        nc.scalar.activation(out=pv[:], in_=vraw[:], func=ACT.Relu)
        lnv = const.tile([P, 1], F32)
        nc.scalar.activation(out=lnv[:], in_=lv[:], func=ACT.Ln, bias=pv[:, 0:1])
        nc.scalar.activation(out=warm[:], in_=one[:], func=ACT.Exp)

        for k in range(5):
            rows_scaled(k)
        tpose(4)
        norms_at = {5: (0, 1), 6: (2, 3), 8: (4, 5), 9: (6, 7)}
        squares_at = {2: (2,), 4: (4,), 6: (6,), 11: (11, 12)}
        colsum_at = {2: 0, 5: 1, 7: 2, 9: 3}
        for i in range(1, 12):
            if i > 1:
                scale(i)
            if i + 4 < ngr:
                tpose(i + 4)
            if i in colsum_at:
                colsum("y", colsum_at[i])
            for t in norms_at.get(i, ()):
                row_norm(t)
            if i == 7:
                take(0)
            if i == 11:
                take(1)
            for w in squares_at.get(i, ()):
                square(w)
        for name, k in (("y", 0), ("x", 0), ("x", 1)):
            quant(name, k)

        sums = [("x", 7, ue) for ue in range(4)] + [("y", g, ue) for g in range(4, 8) for ue in range(4)]
        ends = (4, 7, 11, 15, 19, 20)
        mxu(0)
        row_norm(8)
        row_norm(9)
        square(13)
        square(14)
        for u in range(nun):
            if u + 1 < nun:
                mxu(u + 1)
            addu(u)
            if u < 4:
                scale(12 + u)
            if u < 6:
                for name, g, ue in sums[ends[u - 1] if u else 0:ends[u]]:
                    colsum(name, g, (ue,))
            if u < 2:
                rows_scaled(5 + u)
            if u == 2:
                xrow()
            if u == 3:
                xturn()
            if u == 4:
                take(2)
            if u == 5:
                xtake()
            if u == 6:
                take(3)
            if u >= 1:
                expo(u - 1)
            if u == 1:
                row_norm(10)
                row_norm(11)
                square(15)
            if u == 2:
                row_norm(12)
                row_norm(13)
            if u == 4:
                quant("y", 1)
        expo(nun - 1)
